import numpy as np
import ml_dtypes


def mxq(x, axis, fmt="e4m3"):
    dtype, down = {"e4m3": (ml_dtypes.float8_e4m3fn, 7), "e5m2": (ml_dtypes.float8_e5m2, 14)}[fmt]
    v = np.moveaxis(np.asarray(x, np.float32).astype(ml_dtypes.bfloat16).astype(np.float64), axis, -1)
    blocks = v.reshape(v.shape[:-1] + (-1, 32))
    amax = np.abs(blocks).max(-1, keepdims=True)
    byte = np.maximum(np.where(amax > 0, np.frexp(amax)[1] - 1 + 127, 0) - down, 1)
    scale = np.exp2(byte - 127.0)
    codes = (blocks / scale).astype(np.float32).astype(dtype).astype(np.float64)
    return np.moveaxis((codes * scale).reshape(v.shape), -1, axis)


WIDE = False


def mx_kscale(k):
    if not WIDE:
        return np.ones(k)
    levels = np.array([10, -10, 5, -5, 0])
    a = np.random.permutation(np.resize(levels, k // 512 * 4)).reshape(k // 512, 4)
    idx = np.arange(k)
    return np.exp2(a[idx // 512, idx % 128 // 32])


BF16 = ml_dtypes.bfloat16


def bf(x):
    return np.asarray(x, np.float32).astype(BF16)


def f64(x):
    return np.asarray(x).astype(np.float64)


N, C, H, W, CO, KS, ST = 4, 512, 34, 34, 128, 3, 1
KK = KS * KS
F = C * KK
RUN = np.lcm(KK, 32)


def im2col(x, k, s):
    n, c, h, w = x.shape
    ho = (h - k) // s + 1
    wo = (w - k) // s + 1
    cols = np.stack([x[:, :, i:i + s * (ho - 1) + 1:s, j:j + s * (wo - 1) + 1:s] for i in range(k) for j in range(k)], axis=2)
    cols = cols.transpose(1, 2, 0, 3, 4).reshape(c * k * k, n * ho * wo)
    return cols, (n, ho, wo)


def setup_inputs():
    sc = np.repeat(mx_kscale(F)[::RUN], RUN // KK)
    sf = np.repeat(sc, KK)
    return {"x": bf(np.random.standard_normal((N, C, H, W)) * sc[None, :, None, None]),
            "weight": bf(np.random.uniform(0.0, 1.0, (CO, F)) * 1.7 / np.sqrt(F) / sf[None, :]),
            "bias": bf(np.random.uniform(-1.0, 1.0, (CO, 1)) * 0.5)}


def reference(x, weight, bias):
    cols, (n, ho, wo) = im2col(f64(x), KS, ST)
    flat = (mxq(f64(weight), 1, "e4m3") @ mxq(cols, 0, "e4m3")) + f64(bias)
    return flat.reshape(weight.shape[0], n, ho, wo).transpose(1, 0, 2, 3)

@@ -1,0 +1,138 @@
+from contextlib import ExitStack
+
+import concourse.mybir as mybir
+from concourse.masks import make_identity
+
+F32 = mybir.dt.float32
+BF16 = mybir.dt.bfloat16
+U32 = mybir.dt.uint32
+U8 = mybir.dt.uint8
+FP8X4 = mybir.dt.float8_e4m3fn_x4
+IDENT = mybir.ActivationFunctionType.Identity
+
+P = 128
+NIMG, C, H, W, CO = 4, 512, 34, 34, 128
+TAPS = 9
+PACK = 4
+NT = 8
+G = NT * PACK
+HROWS = 16
+PAIRS = 9
+PAIR_PX = 2 * W
+CALL = 32 * NT
+FLOPS = 2 * CO * C * TAPS * NIMG * 32 * 32
+
+CHUNKS = ((0, 2), (2, 4), (4, 9))
+RING = 28
+
+
+def tile_sparseconv2d_kernel(tc, x, weight, bias, out):
+    nc = tc.nc
+    with ExitStack() as ctx:
+        keep = ctx.enter_context(tc.tile_pool(name="keep", bufs=1))
+        ring = ctx.enter_context(tc.tile_pool(name="ring", bufs=RING))
+        resp = ctx.enter_context(tc.tile_pool(name="resp", bufs=3))
+        accp = ctx.enter_context(tc.psum_pool(name="accp", bufs=3))
+        wpsp = ctx.enter_context(tc.psum_pool(name="wpsp", bufs=5))
+
+        ident = keep.tile([P, P], BF16, name="ident")
+        make_identity(nc, ident[:])
+
+        raws = []
+        w_sb = keep.tile([P, C * TAPS], BF16, name="w_sb")
+        bias_bf = keep.tile([P, 1], BF16, name="bias_bf")
+        nc.scalar.dma_start(out=bias_bf[:], in_=bias)
+        for ci, (p0, p1) in enumerate(CHUNKS):
+            rows = 2 * (p1 - p0)
+            raw = keep.tile([P, G, rows * W], BF16, name="raw%d" % ci)
+            raws.append(raw)
+            for n in range(NIMG):
+                for h in range(2):
+                    g0 = (n * 2 + h) * PACK
+                    r0 = HROWS * h + 2 * p0
+                    nc.sync.dma_start(
+                        out=raw[:, g0:g0 + PACK, :],
+                        in_=x[n, :, r0:r0 + rows, :].rearrange("(p t) r u -> p t (r u)", t=PACK),
+                    )
+            if ci == 1:
+                nc.sync.dma_start(out=w_sb[:], in_=weight)
+
+        bias_f = keep.tile([P, 1], F32, name="bias_f")
+        nc.vector.tensor_copy(out=bias_f[:], in_=bias_bf[:])
+
+        x2 = []
+
+        def regroup(m, eng):
+            ci = [i for i, (p0, p1) in enumerate(CHUNKS) if p0 <= m < p1][0]
+            k = m - CHUNKS[ci][0]
+            dst = keep.tile([P, PAIR_PX * G], BF16, name="x2_%d" % m, align_bytes=64)
+            x2.append(dst)
+            src = raws[ci][:, :, k * PAIR_PX:(k + 1) * PAIR_PX].rearrange("p g (b i) -> p b g i", i=4)
+            dview = dst[:].rearrange("p (b i g) -> p b g i", i=4, g=G)
+            if eng == "v":
+                nc.vector.tensor_copy(out=dview, in_=src)
+            else:
+                nc.scalar.copy(out=dview, in_=src)
+
+        regroup(0, "v")
+        regroup(1, "s")
+
+        wg = keep.tile([P, TAPS, CO, PACK], BF16, name="wg", align_bytes=64)
+        w_codes = keep.tile([P, TAPS * CO], U32, name="w_codes", align_bytes=64)
+        w_scales = keep.tile([P, TAPS * CO], U8, name="w_scales", align_bytes=64)
+        w_view = w_sb[:].rearrange("o (p t k) -> o t k p", t=PACK, k=TAPS)
+        for k0 in range(0, TAPS, 2):
+            nk = min(2, TAPS - k0)
+            wps = wpsp.tile([P, 2 * PACK, CO], BF16, name="wps")
+            for kk in range(nk):
+                for t in range(PACK):
+                    nc.tensor.transpose(wps[:, kk * PACK + t, :], w_view[:, t, k0 + kk, :], ident[:])
+            nc.scalar.copy(
+                out=wg[:, k0:k0 + nk, :, :],
+                in_=wps[:, 0:nk * PACK, :].rearrange("p (k t) o -> p k o t", t=PACK),
+            )
+            nc.vector.quantize_mx(
+                out=w_codes[:, k0 * CO:(k0 + nk) * CO].bitcast(FP8X4),
+                scales=w_scales[:, k0 * CO:(k0 + nk) * CO],
+                in_=wg[:, k0:k0 + nk, :, :].rearrange("p k o t -> p (k o t)"),
+            )
+
+        for m in range(HROWS // 2):
+            if m + 2 < PAIRS:
+                regroup(m + 2, "s")
+            acc = accp.tile([P, 2 * CALL], F32, name="acc")
+            for tap in range(TAPS):
+                i, j = tap // 3, tap % 3
+                codes = ring.tile([P, 2 * CALL], U32, name="codes", align_bytes=64)
+                scales = ring.tile([P, 2 * CALL], U8, name="scales", align_bytes=64)
+                for rr in range(2):
+                    rho = 2 * m + rr + i
+                    e0 = ((rho % 2) * W + j) * G
+                    nc.vector.quantize_mx(
+                        out=codes[:, rr * CALL:(rr + 1) * CALL].bitcast(FP8X4),
+                        scales=scales[:, rr * CALL:(rr + 1) * CALL],
+                        in_=x2[rho // 2][:, e0:e0 + CALL * PACK],
+                    )
+                nc.tensor.matmul_mx(
+                    out=acc[:],
+                    lhsT=w_codes[:, tap * CO:(tap + 1) * CO].bitcast(FP8X4),
+                    lhsT_scale=w_scales[:, tap * CO:(tap + 1) * CO],
+                    rhs=codes[:].bitcast(FP8X4),
+                    rhs_scale=scales[:],
+                    start=(tap == 0),
+                    stop=(tap == TAPS - 1),
+                )
+            res = resp.tile([P, 2 * CALL], F32, name="res")
+            nc.scalar.activation(
+                out=res[:].rearrange("o (g q) -> o g q", g=NT),
+                in_=acc[:].rearrange("o (q g) -> o g q", g=NT),
+                func=IDENT,
+                bias=bias_f[:, 0:1],
+            )
+            rview = res[:].rearrange("o (n h q) -> o n h q", n=NIMG, h=2)
+            for h in range(2):
+                r0 = HROWS * h + 2 * m
+                nc.sync.dma_start(
+                    out=out[:, :, r0:r0 + 2, :].rearrange("n o r u -> o n (r u)"),
+                    in_=rview[:, :, h, :],
+                )

@@ -22,8 +22,12 @@ PAIR_PX = 2 * W
 CALL = 32 * NT
 FLOPS = 2 * CO * C * TAPS * NIMG * 32 * 32
 
-CHUNKS = ((0, 2), (2, 4), (4, 9))
-RING = 28
+CHUNKS = ((0, 2), (2, 3), (3, 5), (5, 9))
+W_AFTER_CHUNK = 0
+RING = 40
+GROUPS = tuple((2 * m, 2 * m + 1) for m in range(7)) + ((14,), (15,))
+W_AFTER = (3, 0)
+AFTER_EVAC = {0: (6,), 2: (7,), 3: (8,)}
 
 
 def tile_sparseconv2d_kernel(tc, x, weight, bias, out):
@@ -37,6 +41,7 @@ def tile_sparseconv2d_kernel(tc, x, weight, bias, out):
 
         ident = keep.tile([P, P], BF16, name="ident")
         make_identity(nc, ident[:])
+        ctx.enter_context(tc.manual_schedule())
 
         raws = []
         w_sb = keep.tile([P, C * TAPS], BF16, name="w_sb")
@@ -54,85 +59,137 @@ def tile_sparseconv2d_kernel(tc, x, weight, bias, out):
                         out=raw[:, g0:g0 + PACK, :],
                         in_=x[n, :, r0:r0 + rows, :].rearrange("(p t) r u -> p t (r u)", t=PACK),
                     )
-            if ci == 1:
+            if ci == W_AFTER_CHUNK:
                 nc.sync.dma_start(out=w_sb[:], in_=weight)
 
-        bias_f = keep.tile([P, 1], F32, name="bias_f")
-        nc.vector.tensor_copy(out=bias_f[:], in_=bias_bf[:])
+        x2 = {}
 
-        x2 = []
-
-        def regroup(m, eng):
+        def regroup(m, on_vector=False):
             ci = [i for i, (p0, p1) in enumerate(CHUNKS) if p0 <= m < p1][0]
             k = m - CHUNKS[ci][0]
             dst = keep.tile([P, PAIR_PX * G], BF16, name="x2_%d" % m, align_bytes=64)
-            x2.append(dst)
+            x2[m] = dst
             src = raws[ci][:, :, k * PAIR_PX:(k + 1) * PAIR_PX].rearrange("p g (b i) -> p b g i", i=4)
             dview = dst[:].rearrange("p (b i g) -> p b g i", i=4, g=G)
-            if eng == "v":
+            if on_vector:
                 nc.vector.tensor_copy(out=dview, in_=src)
             else:
                 nc.scalar.copy(out=dview, in_=src)
-
-        regroup(0, "v")
-        regroup(1, "s")
 
         wg = keep.tile([P, TAPS, CO, PACK], BF16, name="wg", align_bytes=64)
         w_codes = keep.tile([P, TAPS * CO], U32, name="w_codes", align_bytes=64)
         w_scales = keep.tile([P, TAPS * CO], U8, name="w_scales", align_bytes=64)
         w_view = w_sb[:].rearrange("o (p t k) -> o t k p", t=PACK, k=TAPS)
-        for k0 in range(0, TAPS, 2):
+        w_banks = []
+
+        def w_transposes(b):
+            k0 = 2 * b
             nk = min(2, TAPS - k0)
             wps = wpsp.tile([P, 2 * PACK, CO], BF16, name="wps")
+            w_banks.append(wps)
             for kk in range(nk):
                 for t in range(PACK):
                     nc.tensor.transpose(wps[:, kk * PACK + t, :], w_view[:, t, k0 + kk, :], ident[:])
+
+        def w_copy(b):
+            k0 = 2 * b
+            nk = min(2, TAPS - k0)
             nc.scalar.copy(
                 out=wg[:, k0:k0 + nk, :, :],
-                in_=wps[:, 0:nk * PACK, :].rearrange("p (k t) o -> p k o t", t=PACK),
+                in_=w_banks[b][:, 0:nk * PACK, :].rearrange("p (k t) o -> p k o t", t=PACK),
             )
+
+        def w_quantise(b):
+            k0 = 2 * b
+            nk = min(2, TAPS - k0)
             nc.vector.quantize_mx(
                 out=w_codes[:, k0 * CO:(k0 + nk) * CO].bitcast(FP8X4),
                 scales=w_scales[:, k0 * CO:(k0 + nk) * CO],
                 in_=wg[:, k0:k0 + nk, :, :].rearrange("p k o t -> p (k o t)"),
             )
 
-        for m in range(HROWS // 2):
-            if m + 2 < PAIRS:
-                regroup(m + 2, "s")
-            acc = accp.tile([P, 2 * CALL], F32, name="acc")
-            for tap in range(TAPS):
-                i, j = tap // 3, tap % 3
-                codes = ring.tile([P, 2 * CALL], U32, name="codes", align_bytes=64)
-                scales = ring.tile([P, 2 * CALL], U8, name="scales", align_bytes=64)
-                for rr in range(2):
-                    rho = 2 * m + rr + i
-                    e0 = ((rho % 2) * W + j) * G
-                    nc.vector.quantize_mx(
-                        out=codes[:, rr * CALL:(rr + 1) * CALL].bitcast(FP8X4),
-                        scales=scales[:, rr * CALL:(rr + 1) * CALL],
-                        in_=x2[rho // 2][:, e0:e0 + CALL * PACK],
-                    )
+        regroup(0, on_vector=True)
+        regroup(1)
+        for b in range(5):
+            w_transposes(b)
+        w_copy(0)
+        regroup(2)
+        w_copy(1)
+        regroup(3)
+        w_copy(2)
+        w_copy(3)
+        w_copy(4)
+        regroup(4)
+        regroup(5)
+
+        bias_f = keep.tile([P, 1], F32, name="bias_f")
+        accs = {}
+
+        def passes(gi, i, slots):
+            width = len(GROUPS[gi]) * CALL
+            if i == 0:
+                accs[gi] = accp.tile([P, 2 * CALL], F32, name="acc")
+            for j in range(3):
+                tap = 3 * i + j
+                codes, scales = slots[j]
                 nc.tensor.matmul_mx(
-                    out=acc[:],
+                    out=accs[gi][:, 0:width],
                     lhsT=w_codes[:, tap * CO:(tap + 1) * CO].bitcast(FP8X4),
                     lhsT_scale=w_scales[:, tap * CO:(tap + 1) * CO],
-                    rhs=codes[:].bitcast(FP8X4),
-                    rhs_scale=scales[:],
+                    rhs=codes[:, 0:width].bitcast(FP8X4),
+                    rhs_scale=scales[:, 0:width],
                     start=(tap == 0),
                     stop=(tap == TAPS - 1),
                 )
+            if i == 2:
+                finish(gi)
+
+        def finish(gi):
+            rows = GROUPS[gi]
+            width = len(rows) * CALL
             res = resp.tile([P, 2 * CALL], F32, name="res")
             nc.scalar.activation(
-                out=res[:].rearrange("o (g q) -> o g q", g=NT),
-                in_=acc[:].rearrange("o (q g) -> o g q", g=NT),
+                out=res[:, 0:width].rearrange("o (g q) -> o g q", g=NT),
+                in_=accs[gi][:, 0:width].rearrange("o (q g) -> o g q", g=NT),
                 func=IDENT,
                 bias=bias_f[:, 0:1],
             )
-            rview = res[:].rearrange("o (n h q) -> o n h q", n=NIMG, h=2)
+            rview = res[:, 0:width].rearrange("o (n h q) -> o n h q", n=NIMG, h=2)
             for h in range(2):
-                r0 = HROWS * h + 2 * m
-                nc.sync.dma_start(
-                    out=out[:, :, r0:r0 + 2, :].rearrange("n o r u -> o n (r u)"),
+                r0 = HROWS * h + rows[0]
+                eng = nc.scalar if (gi == len(GROUPS) - 1 and h == 1) else nc.sync
+                eng.dma_start(
+                    out=out[:, :, r0:r0 + len(rows), :].rearrange("n o r u -> o n (r u)"),
                     in_=rview[:, :, h, :],
                 )
+            for m in AFTER_EVAC.get(gi, ()):
+                regroup(m)
+
+        pending = []
+        w_ready = False
+        for gi, rows in enumerate(GROUPS):
+            for i in range(3):
+                slots = []
+                for j in range(3):
+                    codes = ring.tile([P, 2 * CALL], U32, name="codes", align_bytes=64)
+                    scales = ring.tile([P, 2 * CALL], U8, name="scales", align_bytes=64)
+                    slots.append((codes, scales))
+                for ri, r in enumerate(rows):
+                    rho = r + i
+                    for j in range(3):
+                        e0 = ((rho % 2) * W + j) * G
+                        nc.vector.quantize_mx(
+                            out=slots[j][0][:, ri * CALL:(ri + 1) * CALL].bitcast(FP8X4),
+                            scales=slots[j][1][:, ri * CALL:(ri + 1) * CALL],
+                            in_=x2[rho // 2][:, e0:e0 + CALL * PACK],
+                        )
+                pending.append((gi, i, slots))
+                if (gi, i) == W_AFTER:
+                    for b in range(5):
+                        w_quantise(b)
+                    nc.vector.tensor_copy(out=bias_f[:], in_=bias_bf[:])
+                    w_ready = True
+                if w_ready:
+                    for item in pending:
+                        passes(item[0], item[1], item[2])
+                    pending = []

@@ -28,6 +28,8 @@ RING = 40
 GROUPS = tuple((2 * m, 2 * m + 1) for m in range(7)) + ((14,), (15,))
 W_AFTER = (3, 0)
 AFTER_EVAC = {0: (6,), 2: (7,), 3: (8,)}
+ROW_PX = 36
+SINGLE_ROWS = 6
 
 
 def tile_sparseconv2d_kernel(tc, x, weight, bias, out):
@@ -47,6 +49,8 @@ def tile_sparseconv2d_kernel(tc, x, weight, bias, out):
         w_sb = keep.tile([P, C * TAPS], BF16, name="w_sb")
         bias_bf = keep.tile([P, 1], BF16, name="bias_bf")
         nc.scalar.dma_start(out=bias_bf[:], in_=bias)
+        bias_f = keep.tile([P, 1], F32, name="bias_f")
+        nc.scalar.activation(out=bias_f[:], in_=bias_bf[:], func=IDENT)
         for ci, (p0, p1) in enumerate(CHUNKS):
             rows = 2 * (p1 - p0)
             raw = keep.tile([P, G, rows * W], BF16, name="raw%d" % ci)
@@ -76,6 +80,28 @@ def tile_sparseconv2d_kernel(tc, x, weight, bias, out):
             else:
                 nc.scalar.copy(out=dview, in_=src)
 
+        xrow = {}
+
+        def regroup_row(rho, on_vector=False):
+            m = rho // 2
+            ci = [i for i, (p0, p1) in enumerate(CHUNKS) if p0 <= m < p1][0]
+            px0 = (m - CHUNKS[ci][0]) * PAIR_PX + (rho % 2) * (PAIR_PX - ROW_PX)
+            dst = keep.tile([P, ROW_PX * G], BF16, name="xrow_%d" % rho, align_bytes=64)
+            xrow[rho] = dst
+            src = raws[ci][:, :, px0:px0 + ROW_PX].rearrange("p g (b i) -> p b g i", i=4)
+            dview = dst[:].rearrange("p (b i g) -> p b g i", i=4, g=G)
+            if on_vector:
+                nc.vector.tensor_copy(out=dview, in_=src)
+            else:
+                nc.scalar.copy(out=dview, in_=src)
+
+        def window(rho, j):
+            if rho < SINGLE_ROWS:
+                e0 = ((rho % 2) * (W - (PAIR_PX - ROW_PX)) + j) * G
+                return xrow[rho][:, e0:e0 + CALL * PACK]
+            e0 = ((rho % 2) * W + j) * G
+            return x2[rho // 2][:, e0:e0 + CALL * PACK]
+
         wg = keep.tile([P, TAPS, CO, PACK], BF16, name="wg", align_bytes=64)
         w_codes = keep.tile([P, TAPS * CO], U32, name="w_codes", align_bytes=64)
         w_scales = keep.tile([P, TAPS * CO], U8, name="w_scales", align_bytes=64)
@@ -99,21 +125,22 @@ def tile_sparseconv2d_kernel(tc, x, weight, bias, out):
                 in_=w_banks[b][:, 0:nk * PACK, :].rearrange("p (k t) o -> p k o t", t=PACK),
             )
 
-        def w_quantise(b):
-            k0 = 2 * b
-            nk = min(2, TAPS - k0)
+        def w_quantise(k0, nk):
             nc.vector.quantize_mx(
                 out=w_codes[:, k0 * CO:(k0 + nk) * CO].bitcast(FP8X4),
                 scales=w_scales[:, k0 * CO:(k0 + nk) * CO],
                 in_=wg[:, k0:k0 + nk, :, :].rearrange("p k o t -> p (k o t)"),
             )
 
-        regroup(0, on_vector=True)
-        regroup(1)
+        regroup_row(0, on_vector=True)
+        regroup_row(1)
+        regroup_row(2)
+        regroup_row(3)
         for b in range(5):
             w_transposes(b)
         w_copy(0)
-        regroup(2)
+        regroup_row(4)
+        regroup_row(5)
         w_copy(1)
         regroup(3)
         w_copy(2)
@@ -122,7 +149,6 @@ def tile_sparseconv2d_kernel(tc, x, weight, bias, out):
         regroup(4)
         regroup(5)
 
-        bias_f = keep.tile([P, 1], F32, name="bias_f")
         accs = {}
 
         def passes(gi, i, slots):
@@ -177,17 +203,15 @@ def tile_sparseconv2d_kernel(tc, x, weight, bias, out):
                 for ri, r in enumerate(rows):
                     rho = r + i
                     for j in range(3):
-                        e0 = ((rho % 2) * W + j) * G
                         nc.vector.quantize_mx(
                             out=slots[j][0][:, ri * CALL:(ri + 1) * CALL].bitcast(FP8X4),
                             scales=slots[j][1][:, ri * CALL:(ri + 1) * CALL],
-                            in_=x2[rho // 2][:, e0:e0 + CALL * PACK],
+                            in_=window(rho, j),
                         )
                 pending.append((gi, i, slots))
                 if (gi, i) == W_AFTER:
-                    for b in range(5):
-                        w_quantise(b)
-                    nc.vector.tensor_copy(out=bias_f[:], in_=bias_bf[:])
+                    w_quantise(0, 8)
+                    w_quantise(8, 1)
                     w_ready = True
                 if w_ready:
                     for item in pending:

@@ -28,8 +28,8 @@ RING = 40
 GROUPS = tuple((2 * m, 2 * m + 1) for m in range(7)) + ((14,), (15,))
 W_AFTER = (3, 0)
 AFTER_EVAC = {0: (6,), 2: (7,), 3: (8,)}
-ROW_PX = 36
-SINGLE_ROWS = 6
+HEAD_ROWS = 4
+HEAD_ORDER = (4, 5, 6, 7, 0, 1, 2, 3)
 
 
 def tile_sparseconv2d_kernel(tc, x, weight, bias, out):
@@ -55,14 +55,13 @@ def tile_sparseconv2d_kernel(tc, x, weight, bias, out):
             rows = 2 * (p1 - p0)
             raw = keep.tile([P, G, rows * W], BF16, name="raw%d" % ci)
             raws.append(raw)
-            for n in range(NIMG):
-                for h in range(2):
-                    g0 = (n * 2 + h) * PACK
-                    r0 = HROWS * h + 2 * p0
-                    nc.sync.dma_start(
-                        out=raw[:, g0:g0 + PACK, :],
-                        in_=x[n, :, r0:r0 + rows, :].rearrange("(p t) r u -> p t (r u)", t=PACK),
-                    )
+            for tau in HEAD_ORDER:
+                n, h = tau // 2, tau % 2
+                r0 = HROWS * h + 2 * p0
+                nc.sync.dma_start(
+                    out=raw[:, tau * PACK:(tau + 1) * PACK, :],
+                    in_=x[n, :, r0:r0 + rows, :].rearrange("(p t) r u -> p t (r u)", t=PACK),
+                )
             if ci == W_AFTER_CHUNK:
                 nc.sync.dma_start(out=w_sb[:], in_=weight)
 
@@ -80,25 +79,20 @@ def tile_sparseconv2d_kernel(tc, x, weight, bias, out):
             else:
                 nc.scalar.copy(out=dview, in_=src)
 
-        xrow = {}
+        x2_head = keep.tile([P, HEAD_ROWS * W * G], BF16, name="x2_head", align_bytes=64)
 
-        def regroup_row(rho, on_vector=False):
-            m = rho // 2
-            ci = [i for i, (p0, p1) in enumerate(CHUNKS) if p0 <= m < p1][0]
-            px0 = (m - CHUNKS[ci][0]) * PAIR_PX + (rho % 2) * (PAIR_PX - ROW_PX)
-            dst = keep.tile([P, ROW_PX * G], BF16, name="xrow_%d" % rho, align_bytes=64)
-            xrow[rho] = dst
-            src = raws[ci][:, :, px0:px0 + ROW_PX].rearrange("p g (b i) -> p b g i", i=4)
-            dview = dst[:].rearrange("p (b i g) -> p b g i", i=4, g=G)
-            if on_vector:
+        def regroup_head_tile(tau):
+            src = raws[0][:, tau * PACK:(tau + 1) * PACK, :].rearrange("p t q -> p q t")
+            dview = x2_head[:].rearrange("p (q g t) -> p q g t", g=NT, t=PACK)[:, :, tau, :]
+            if tau < NT // 2:
                 nc.vector.tensor_copy(out=dview, in_=src)
             else:
                 nc.scalar.copy(out=dview, in_=src)
 
         def window(rho, j):
-            if rho < SINGLE_ROWS:
-                e0 = ((rho % 2) * (W - (PAIR_PX - ROW_PX)) + j) * G
-                return xrow[rho][:, e0:e0 + CALL * PACK]
+            if rho < HEAD_ROWS:
+                e0 = (rho * W + j) * G
+                return x2_head[:, e0:e0 + CALL * PACK]
             e0 = ((rho % 2) * W + j) * G
             return x2[rho // 2][:, e0:e0 + CALL * PACK]
 
@@ -132,15 +126,12 @@ def tile_sparseconv2d_kernel(tc, x, weight, bias, out):
                 in_=wg[:, k0:k0 + nk, :, :].rearrange("p k o t -> p (k o t)"),
             )
 
-        regroup_row(0, on_vector=True)
-        regroup_row(1)
-        regroup_row(2)
-        regroup_row(3)
+        for tau in HEAD_ORDER:
+            regroup_head_tile(tau)
         for b in range(5):
             w_transposes(b)
         w_copy(0)
-        regroup_row(4)
-        regroup_row(5)
+        regroup(2)
         w_copy(1)
         regroup(3)
         w_copy(2)

@@ -29,7 +29,7 @@ GROUPS = tuple((2 * m, 2 * m + 1) for m in range(7)) + ((14,), (15,))
 W_AFTER = (3, 0)
 AFTER_EVAC = {0: (6,), 2: (7,), 3: (8,)}
 HEAD_ROWS = 4
-HEAD_ORDER = (4, 5, 6, 7, 0, 1, 2, 3)
+HEAD_IMAGES = (2, 3, 0, 1)
 
 
 def tile_sparseconv2d_kernel(tc, x, weight, bias, out):
@@ -49,13 +49,14 @@ def tile_sparseconv2d_kernel(tc, x, weight, bias, out):
         w_sb = keep.tile([P, C * TAPS], BF16, name="w_sb")
         bias_bf = keep.tile([P, 1], BF16, name="bias_bf")
         nc.scalar.dma_start(out=bias_bf[:], in_=bias)
-        bias_f = keep.tile([P, 1], F32, name="bias_f")
-        nc.scalar.activation(out=bias_f[:], in_=bias_bf[:], func=IDENT)
+        warm = keep.tile([P, 2], F32, name="warm")
+        nc.vector.memset(warm[:, 0:1], 0.0)
+        nc.scalar.activation(out=warm[:, 1:2], in_=warm[:, 0:1], func=IDENT)
         for ci, (p0, p1) in enumerate(CHUNKS):
             rows = 2 * (p1 - p0)
             raw = keep.tile([P, G, rows * W], BF16, name="raw%d" % ci)
             raws.append(raw)
-            for tau in HEAD_ORDER:
+            for tau in [2 * n + h for n in (HEAD_IMAGES if ci == 0 else range(NIMG)) for h in range(2)]:
                 n, h = tau // 2, tau % 2
                 r0 = HROWS * h + 2 * p0
                 nc.sync.dma_start(
@@ -81,10 +82,11 @@ def tile_sparseconv2d_kernel(tc, x, weight, bias, out):
 
         x2_head = keep.tile([P, HEAD_ROWS * W * G], BF16, name="x2_head", align_bytes=64)
 
-        def regroup_head_tile(tau):
-            src = raws[0][:, tau * PACK:(tau + 1) * PACK, :].rearrange("p t q -> p q t")
-            dview = x2_head[:].rearrange("p (q g t) -> p q g t", g=NT, t=PACK)[:, :, tau, :]
-            if tau < NT // 2:
+        def regroup_image(ci, dst, n, on_vector):
+            gi = 2 * PACK
+            src = raws[ci][:, n * gi:(n + 1) * gi, :].rearrange("p g (b i) -> p b g i", i=4)
+            dview = dst[:].rearrange("p (b i m g) -> p m b g i", i=4, m=NIMG, g=gi)[:, n]
+            if on_vector:
                 nc.vector.tensor_copy(out=dview, in_=src)
             else:
                 nc.scalar.copy(out=dview, in_=src)
@@ -126,15 +128,17 @@ def tile_sparseconv2d_kernel(tc, x, weight, bias, out):
                 in_=wg[:, k0:k0 + nk, :, :].rearrange("p k o t -> p (k o t)"),
             )
 
-        for tau in HEAD_ORDER:
-            regroup_head_tile(tau)
+        for n in HEAD_IMAGES:
+            regroup_image(0, x2_head, n, n < 2)
         for b in range(5):
             w_transposes(b)
+        x2[2] = keep.tile([P, PAIR_PX * G], BF16, name="x2_2", align_bytes=64)
+        for n in range(NIMG):
+            regroup_image(1, x2[2], n, False)
         w_copy(0)
-        regroup(2)
         w_copy(1)
-        regroup(3)
         w_copy(2)
+        regroup(3)
         w_copy(3)
         w_copy(4)
         regroup(4)
@@ -169,7 +173,7 @@ def tile_sparseconv2d_kernel(tc, x, weight, bias, out):
                 out=res[:, 0:width].rearrange("o (g q) -> o g q", g=NT),
                 in_=accs[gi][:, 0:width].rearrange("o (q g) -> o g q", g=NT),
                 func=IDENT,
-                bias=bias_f[:, 0:1],
+                bias=bias_bf[:, 0:1],
             )
             rview = res[:, 0:width].rearrange("o (n h q) -> o n h q", n=NIMG, h=2)
             for h in range(2):

@@ -54,13 +54,14 @@ def tile_sparseconv2d_kernel(tc, x, weight, bias, out):
         nc.scalar.activation(out=warm[:, 1:2], in_=warm[:, 0:1], func=IDENT)
         for ci, (p0, p1) in enumerate(CHUNKS):
             rows = 2 * (p1 - p0)
-            raw = keep.tile([P, G, rows * W], BF16, name="raw%d" % ci)
+            pitch = -(-rows * W // 16) * 16
+            raw = keep.tile([P, G, pitch], BF16, name="raw%d" % ci)
             raws.append(raw)
             for tau in [2 * n + h for n in (HEAD_IMAGES if ci == 0 else range(NIMG)) for h in range(2)]:
                 n, h = tau // 2, tau % 2
                 r0 = HROWS * h + 2 * p0
                 nc.sync.dma_start(
-                    out=raw[:, tau * PACK:(tau + 1) * PACK, :],
+                    out=raw[:, tau * PACK:(tau + 1) * PACK, 0:rows * W],
                     in_=x[n, :, r0:r0 + rows, :].rearrange("(p t) r u -> p t (r u)", t=PACK),
                 )
             if ci == W_AFTER_CHUNK:
@@ -84,7 +85,8 @@ def tile_sparseconv2d_kernel(tc, x, weight, bias, out):
 
         def regroup_image(ci, dst, n, on_vector):
             gi = 2 * PACK
-            src = raws[ci][:, n * gi:(n + 1) * gi, :].rearrange("p g (b i) -> p b g i", i=4)
+            npx = 2 * W * (CHUNKS[ci][1] - CHUNKS[ci][0])
+            src = raws[ci][:, n * gi:(n + 1) * gi, 0:npx].rearrange("p g (b i) -> p b g i", i=4)
             dview = dst[:].rearrange("p (b i m g) -> p m b g i", i=4, m=NIMG, g=gi)[:, n]
             if on_vector:
                 nc.vector.tensor_copy(out=dview, in_=src)

@@ -26,7 +26,7 @@ CHUNKS = ((0, 2), (2, 3), (3, 5), (5, 9))
 W_AFTER_CHUNK = 0
 RING = 40
 GROUPS = tuple((2 * m, 2 * m + 1) for m in range(7)) + ((14,), (15,))
-W_AFTER = (3, 0)
+W_AFTER = (3, 2)
 AFTER_EVAC = {0: (6,), 2: (7,), 3: (8,)}
 HEAD_ROWS = 4
 HEAD_IMAGES = (2, 3, 0, 1)
@@ -83,10 +83,9 @@ def tile_sparseconv2d_kernel(tc, x, weight, bias, out):
 
         x2_head = keep.tile([P, HEAD_ROWS * W * G], BF16, name="x2_head", align_bytes=64)
 
-        def regroup_image(ci, dst, n, on_vector):
+        def regroup_image(ci, npairs, dst, n, on_vector):
             gi = 2 * PACK
-            npx = 2 * W * (CHUNKS[ci][1] - CHUNKS[ci][0])
-            src = raws[ci][:, n * gi:(n + 1) * gi, 0:npx].rearrange("p g (b i) -> p b g i", i=4)
+            src = raws[ci][:, n * gi:(n + 1) * gi, 0:npairs * PAIR_PX].rearrange("p g (b i) -> p b g i", i=4)
             dview = dst[:].rearrange("p (b i m g) -> p m b g i", i=4, m=NIMG, g=gi)[:, n]
             if on_vector:
                 nc.vector.tensor_copy(out=dview, in_=src)
@@ -131,19 +130,21 @@ def tile_sparseconv2d_kernel(tc, x, weight, bias, out):
             )
 
         for n in HEAD_IMAGES:
-            regroup_image(0, x2_head, n, n < 2)
+            regroup_image(0, 2, x2_head, n, n < 2)
         for b in range(5):
             w_transposes(b)
         x2[2] = keep.tile([P, PAIR_PX * G], BF16, name="x2_2", align_bytes=64)
         for n in range(NIMG):
-            regroup_image(1, x2[2], n, False)
+            regroup_image(1, 1, x2[2], n, False)
         w_copy(0)
+        x2[3] = keep.tile([P, PAIR_PX * G], BF16, name="x2_3", align_bytes=64)
+        for n in range(NIMG):
+            regroup_image(2, 1, x2[3], n, False)
         w_copy(1)
         w_copy(2)
-        regroup(3)
+        regroup(4)
         w_copy(3)
         w_copy(4)
-        regroup(4)
         regroup(5)
 
         accs = {}

@@ -8,210 +8,215 @@ BF16 = mybir.dt.bfloat16
 U32 = mybir.dt.uint32
 U8 = mybir.dt.uint8
 FP8X4 = mybir.dt.float8_e4m3fn_x4
-IDENT = mybir.ActivationFunctionType.Identity
+IDENTITY = mybir.ActivationFunctionType.Identity
 
 P = 128
-NIMG, C, H, W, CO = 4, 512, 34, 34, 128
+IMAGES, CHANNELS, WIDTH, OUT_CH = 4, 512, 34, 128
+OUT_WIDTH = WIDTH - 2
 TAPS = 9
 PACK = 4
-NT = 8
-G = NT * PACK
-HROWS = 16
-PAIRS = 9
-PAIR_PX = 2 * W
-CALL = 32 * NT
-FLOPS = 2 * CO * C * TAPS * NIMG * 32 * 32
+STRIPS = 2 * IMAGES
+STRIP_ROWS = 16
+LANES = STRIPS * PACK
+IMAGE_LANES = 2 * PACK
+PAIR = 2 * WIDTH
+RUN = 4
+COLS = OUT_WIDTH * STRIPS
+FLOPS = 2 * OUT_CH * CHANNELS * TAPS * IMAGES * OUT_WIDTH * OUT_WIDTH
 
 CHUNKS = ((0, 2), (2, 3), (3, 5), (5, 9))
-W_AFTER_CHUNK = 0
-RING = 40
-GROUPS = tuple((2 * m, 2 * m + 1) for m in range(7)) + ((14,), (15,))
-W_AFTER = (3, 2)
-AFTER_EVAC = {0: (6,), 2: (7,), 3: (8,)}
-HEAD_ROWS = 4
+HEAD_PAIRS = CHUNKS[0][1]
 HEAD_IMAGES = (2, 3, 0, 1)
+GROUPS = tuple((r, r + 1) for r in range(0, STRIP_ROWS - 2, 2)) + ((STRIP_ROWS - 2,), (STRIP_ROWS - 1,))
+WEIGHTS_AFTER = (3, 0)
+SLOTS = 40
+REGROUP_AFTER_GROUP = {0: (6,), 2: (7,), 3: (8,)}
+TAPS_PER_BANK = 2
+WEIGHT_BANKS = 5
 
 
 def tile_sparseconv2d_kernel(tc, x, weight, bias, out):
     nc = tc.nc
     with ExitStack() as ctx:
         keep = ctx.enter_context(tc.tile_pool(name="keep", bufs=1))
-        ring = ctx.enter_context(tc.tile_pool(name="ring", bufs=RING))
-        resp = ctx.enter_context(tc.tile_pool(name="resp", bufs=3))
-        accp = ctx.enter_context(tc.psum_pool(name="accp", bufs=3))
-        wpsp = ctx.enter_context(tc.psum_pool(name="wpsp", bufs=5))
+        slots_pool = ctx.enter_context(tc.tile_pool(name="slots", bufs=SLOTS))
+        result_pool = ctx.enter_context(tc.tile_pool(name="result", bufs=3))
+        sums_pool = ctx.enter_context(tc.psum_pool(name="sums", bufs=3))
+        weight_psum = ctx.enter_context(tc.psum_pool(name="weight_psum", bufs=WEIGHT_BANKS))
 
-        ident = keep.tile([P, P], BF16, name="ident")
-        make_identity(nc, ident[:])
+        identity = keep.tile([P, P], BF16, name="identity")
+        make_identity(nc, identity[:])
+
         ctx.enter_context(tc.manual_schedule())
 
-        raws = []
-        w_sb = keep.tile([P, C * TAPS], BF16, name="w_sb")
-        bias_bf = keep.tile([P, 1], BF16, name="bias_bf")
-        nc.scalar.dma_start(out=bias_bf[:], in_=bias)
+        weight_rows = keep.tile([P, CHANNELS * TAPS], BF16, name="weight_rows")
+        bias_col = keep.tile([P, 1], BF16, name="bias_col")
+
         warm = keep.tile([P, 2], F32, name="warm")
         nc.vector.memset(warm[:, 0:1], 0.0)
-        nc.scalar.activation(out=warm[:, 1:2], in_=warm[:, 0:1], func=IDENT)
-        for ci, (p0, p1) in enumerate(CHUNKS):
-            rows = 2 * (p1 - p0)
-            pitch = -(-rows * W // 16) * 16
-            raw = keep.tile([P, G, pitch], BF16, name="raw%d" % ci)
-            raws.append(raw)
-            for tau in [2 * n + h for n in (HEAD_IMAGES if ci == 0 else range(NIMG)) for h in range(2)]:
-                n, h = tau // 2, tau % 2
-                r0 = HROWS * h + 2 * p0
+        nc.scalar.activation(out=warm[:, 1:2], in_=warm[:, 0:1], func=IDENTITY)
+
+        staged = []
+        for chunk, (first_pair, end_pair) in enumerate(CHUNKS):
+            rows = 2 * (end_pair - first_pair)
+            pitch = -(-rows * WIDTH // 16) * 16
+            lanes = keep.tile([P, LANES, pitch], BF16, name="staged%d" % chunk)
+            staged.append(lanes)
+            for strip in [2 * n + h for n in (HEAD_IMAGES if chunk == 0 else range(IMAGES)) for h in range(2)]:
+                n, h = strip // 2, strip % 2
+                row0 = STRIP_ROWS * h + 2 * first_pair
                 nc.sync.dma_start(
-                    out=raw[:, tau * PACK:(tau + 1) * PACK, 0:rows * W],
-                    in_=x[n, :, r0:r0 + rows, :].rearrange("(p t) r u -> p t (r u)", t=PACK),
+                    out=lanes[:, strip * PACK:(strip + 1) * PACK, 0:rows * WIDTH],
+                    in_=x[n, :, row0:row0 + rows, :].rearrange("(p t) r u -> p t (r u)", t=PACK),
                 )
-            if ci == W_AFTER_CHUNK:
-                nc.sync.dma_start(out=w_sb[:], in_=weight)
+            if chunk == 0:
+                nc.sync.dma_start(out=weight_rows[:], in_=weight)
+        nc.sync.dma_start(out=bias_col[:], in_=bias)
 
-        x2 = {}
+        spread = {}
 
-        def regroup(m, on_vector=False):
-            ci = [i for i, (p0, p1) in enumerate(CHUNKS) if p0 <= m < p1][0]
-            k = m - CHUNKS[ci][0]
-            dst = keep.tile([P, PAIR_PX * G], BF16, name="x2_%d" % m, align_bytes=64)
-            x2[m] = dst
-            src = raws[ci][:, :, k * PAIR_PX:(k + 1) * PAIR_PX].rearrange("p g (b i) -> p b g i", i=4)
-            dview = dst[:].rearrange("p (b i g) -> p b g i", i=4, g=G)
-            if on_vector:
-                nc.vector.tensor_copy(out=dview, in_=src)
-            else:
-                nc.scalar.copy(out=dview, in_=src)
+        def regroup(chunk, target, position0, positions, lane0, lanes, engine_copy):
+            source = staged[chunk][:, lane0:lane0 + lanes, position0:position0 + positions]
+            engine_copy(
+                out=target.rearrange("p (b i m g) -> p m b g i", i=RUN, m=LANES // lanes, g=lanes)[:, lane0 // lanes],
+                in_=source.rearrange("p g (b i) -> p b g i", i=RUN),
+            )
 
-        x2_head = keep.tile([P, HEAD_ROWS * W * G], BF16, name="x2_head", align_bytes=64)
+        def new_pair(pair):
+            spread[pair] = keep.tile([P, PAIR * LANES], BF16, name="spread%d" % pair, align_bytes=64)
+            chunk = [k for k, (first, end) in enumerate(CHUNKS) if first <= pair < end][0]
+            return chunk, (pair - CHUNKS[chunk][0]) * PAIR
 
-        def regroup_image(ci, npairs, dst, n, on_vector):
-            gi = 2 * PACK
-            src = raws[ci][:, n * gi:(n + 1) * gi, 0:npairs * PAIR_PX].rearrange("p g (b i) -> p b g i", i=4)
-            dview = dst[:].rearrange("p (b i m g) -> p m b g i", i=4, m=NIMG, g=gi)[:, n]
-            if on_vector:
-                nc.vector.tensor_copy(out=dview, in_=src)
-            else:
-                nc.scalar.copy(out=dview, in_=src)
+        def regroup_pair(pair):
+            chunk, position0 = new_pair(pair)
+            regroup(chunk, spread[pair][:], position0, PAIR, 0, LANES, nc.scalar.copy)
 
-        def window(rho, j):
-            if rho < HEAD_ROWS:
-                e0 = (rho * W + j) * G
-                return x2_head[:, e0:e0 + CALL * PACK]
-            e0 = ((rho % 2) * W + j) * G
-            return x2[rho // 2][:, e0:e0 + CALL * PACK]
+        def regroup_pair_by_image(pair):
+            chunk, position0 = new_pair(pair)
+            for n in range(IMAGES):
+                regroup(chunk, spread[pair][:], position0, PAIR, n * IMAGE_LANES, IMAGE_LANES, nc.scalar.copy)
 
-        wg = keep.tile([P, TAPS, CO, PACK], BF16, name="wg", align_bytes=64)
-        w_codes = keep.tile([P, TAPS * CO], U32, name="w_codes", align_bytes=64)
-        w_scales = keep.tile([P, TAPS * CO], U8, name="w_scales", align_bytes=64)
-        w_view = w_sb[:].rearrange("o (p t k) -> o t k p", t=PACK, k=TAPS)
-        w_banks = []
+        head = keep.tile([P, HEAD_PAIRS * PAIR * LANES], BF16, name="head", align_bytes=64)
 
-        def w_transposes(b):
-            k0 = 2 * b
-            nk = min(2, TAPS - k0)
-            wps = wpsp.tile([P, 2 * PACK, CO], BF16, name="wps")
-            w_banks.append(wps)
-            for kk in range(nk):
+        def window(row, j):
+            if row < 2 * HEAD_PAIRS:
+                start = (row * WIDTH + j) * LANES
+                return head[:, start:start + COLS * PACK]
+            start = ((row % 2) * WIDTH + j) * LANES
+            return spread[row // 2][:, start:start + COLS * PACK]
+
+        grouped = keep.tile([P, TAPS, OUT_CH, PACK], BF16, name="grouped", align_bytes=64)
+        weight_codes = keep.tile([P, TAPS * OUT_CH], U32, name="weight_codes", align_bytes=64)
+        weight_scales = keep.tile([P, TAPS * OUT_CH], U8, name="weight_scales", align_bytes=64)
+        by_tap = weight_rows[:].rearrange("o (p t k) -> o t k p", t=PACK, k=TAPS)
+        banks = []
+
+        def transpose_weights(bank):
+            tap0 = TAPS_PER_BANK * bank
+            turned = weight_psum.tile([P, TAPS_PER_BANK * PACK, OUT_CH], BF16, name="turned")
+            banks.append(turned)
+            for k in range(min(TAPS_PER_BANK, TAPS - tap0)):
                 for t in range(PACK):
-                    nc.tensor.transpose(wps[:, kk * PACK + t, :], w_view[:, t, k0 + kk, :], ident[:])
+                    nc.tensor.transpose(turned[:, k * PACK + t, :], by_tap[:, t, tap0 + k, :], identity[:])
 
-        def w_copy(b):
-            k0 = 2 * b
-            nk = min(2, TAPS - k0)
+        def group_weights(bank):
+            tap0 = TAPS_PER_BANK * bank
+            taps = min(TAPS_PER_BANK, TAPS - tap0)
             nc.scalar.copy(
-                out=wg[:, k0:k0 + nk, :, :],
-                in_=w_banks[b][:, 0:nk * PACK, :].rearrange("p (k t) o -> p k o t", t=PACK),
+                out=grouped[:, tap0:tap0 + taps, :, :],
+                in_=banks[bank][:, 0:taps * PACK, :].rearrange("p (k t) o -> p k o t", t=PACK),
             )
 
-        def w_quantise(k0, nk):
+        def quantise_weights(tap0, taps):
             nc.vector.quantize_mx(
-                out=w_codes[:, k0 * CO:(k0 + nk) * CO].bitcast(FP8X4),
-                scales=w_scales[:, k0 * CO:(k0 + nk) * CO],
-                in_=wg[:, k0:k0 + nk, :, :].rearrange("p k o t -> p (k o t)"),
+                out=weight_codes[:, tap0 * OUT_CH:(tap0 + taps) * OUT_CH].bitcast(FP8X4),
+                scales=weight_scales[:, tap0 * OUT_CH:(tap0 + taps) * OUT_CH],
+                in_=grouped[:, tap0:tap0 + taps, :, :].rearrange("p k o t -> p (k o t)"),
             )
 
-        for n in HEAD_IMAGES:
-            regroup_image(0, 2, x2_head, n, n < 2)
-        for b in range(5):
-            w_transposes(b)
-        x2[2] = keep.tile([P, PAIR_PX * G], BF16, name="x2_2", align_bytes=64)
-        for n in range(NIMG):
-            regroup_image(1, 1, x2[2], n, False)
-        w_copy(0)
-        x2[3] = keep.tile([P, PAIR_PX * G], BF16, name="x2_3", align_bytes=64)
-        for n in range(NIMG):
-            regroup_image(2, 1, x2[3], n, False)
-        w_copy(1)
-        w_copy(2)
-        regroup(4)
-        w_copy(3)
-        w_copy(4)
-        regroup(5)
+        head_positions = HEAD_PAIRS * PAIR
+        regroup(0, head[:], 0, head_positions, 2 * IMAGE_LANES, IMAGE_LANES, nc.scalar.copy)
+        regroup(0, head[:], 0, head_positions, 3 * IMAGE_LANES, IMAGE_LANES, nc.scalar.copy)
+        regroup(0, head[:, 0:PAIR * LANES], 0, PAIR, 0, IMAGE_LANES, nc.vector.tensor_copy)
+        regroup(0, head[:, 0:PAIR * LANES], 0, PAIR, IMAGE_LANES, IMAGE_LANES, nc.vector.tensor_copy)
+        regroup(0, head[:, PAIR * LANES:2 * PAIR * LANES], PAIR, PAIR, 0, 2 * IMAGE_LANES, nc.scalar.copy)
 
-        accs = {}
+        for bank in range(WEIGHT_BANKS):
+            transpose_weights(bank)
 
-        def passes(gi, i, slots):
-            width = len(GROUPS[gi]) * CALL
+        regroup_pair_by_image(2)
+        group_weights(0)
+        group_weights(1)
+        group_weights(2)
+        regroup_pair(3)
+        group_weights(3)
+        group_weights(4)
+        regroup_pair(4)
+        regroup_pair(5)
+
+        sums = {}
+
+        def multiply(group, i, operands):
+            width = len(GROUPS[group]) * COLS
             if i == 0:
-                accs[gi] = accp.tile([P, 2 * CALL], F32, name="acc")
+                sums[group] = sums_pool.tile([P, 2 * COLS], F32, name="sums")
             for j in range(3):
                 tap = 3 * i + j
-                codes, scales = slots[j]
+                codes, scales = operands[j]
                 nc.tensor.matmul_mx(
-                    out=accs[gi][:, 0:width],
-                    lhsT=w_codes[:, tap * CO:(tap + 1) * CO].bitcast(FP8X4),
-                    lhsT_scale=w_scales[:, tap * CO:(tap + 1) * CO],
+                    out=sums[group][:, 0:width],
+                    lhsT=weight_codes[:, tap * OUT_CH:(tap + 1) * OUT_CH].bitcast(FP8X4),
+                    lhsT_scale=weight_scales[:, tap * OUT_CH:(tap + 1) * OUT_CH],
                     rhs=codes[:, 0:width].bitcast(FP8X4),
                     rhs_scale=scales[:, 0:width],
                     start=(tap == 0),
                     stop=(tap == TAPS - 1),
                 )
             if i == 2:
-                finish(gi)
+                finish(group)
 
-        def finish(gi):
-            rows = GROUPS[gi]
-            width = len(rows) * CALL
-            res = resp.tile([P, 2 * CALL], F32, name="res")
+        def finish(group):
+            rows = GROUPS[group]
+            width = len(rows) * COLS
+            result = result_pool.tile([P, 2 * COLS], F32, name="result")
             nc.scalar.activation(
-                out=res[:, 0:width].rearrange("o (g q) -> o g q", g=NT),
-                in_=accs[gi][:, 0:width].rearrange("o (q g) -> o g q", g=NT),
-                func=IDENT,
-                bias=bias_bf[:, 0:1],
+                out=result[:, 0:width].rearrange("o (s q) -> o s q", s=STRIPS),
+                in_=sums[group][:, 0:width].rearrange("o (q s) -> o s q", s=STRIPS),
+                func=IDENTITY,
+                bias=bias_col[:, 0:1],
             )
-            rview = res[:, 0:width].rearrange("o (n h q) -> o n h q", n=NIMG, h=2)
+            by_half = result[:, 0:width].rearrange("o (n h q) -> o n h q", n=IMAGES, h=2)
             for h in range(2):
-                r0 = HROWS * h + rows[0]
-                eng = nc.scalar if (gi == len(GROUPS) - 1 and h == 1) else nc.sync
-                eng.dma_start(
-                    out=out[:, :, r0:r0 + len(rows), :].rearrange("n o r u -> o n (r u)"),
-                    in_=rview[:, :, h, :],
+                row0 = STRIP_ROWS * h + rows[0]
+                nc.sync.dma_start(
+                    out=out[:, :, row0:row0 + len(rows), :].rearrange("n o r u -> o n (r u)"),
+                    in_=by_half[:, :, h, :],
                 )
-            for m in AFTER_EVAC.get(gi, ()):
-                regroup(m)
+            for pair in REGROUP_AFTER_GROUP.get(group, ()):
+                regroup_pair(pair)
 
-        pending = []
-        w_ready = False
-        for gi, rows in enumerate(GROUPS):
+        waiting = []
+        weights_ready = False
+        for group, rows in enumerate(GROUPS):
             for i in range(3):
-                slots = []
+                operands = []
                 for j in range(3):
-                    codes = ring.tile([P, 2 * CALL], U32, name="codes", align_bytes=64)
-                    scales = ring.tile([P, 2 * CALL], U8, name="scales", align_bytes=64)
-                    slots.append((codes, scales))
-                for ri, r in enumerate(rows):
-                    rho = r + i
+                    codes = slots_pool.tile([P, 2 * COLS], U32, name="codes", align_bytes=64)
+                    scales = slots_pool.tile([P, 2 * COLS], U8, name="scales", align_bytes=64)
+                    operands.append((codes, scales))
+                for k, r in enumerate(rows):
                     for j in range(3):
                         nc.vector.quantize_mx(
-                            out=slots[j][0][:, ri * CALL:(ri + 1) * CALL].bitcast(FP8X4),
-                            scales=slots[j][1][:, ri * CALL:(ri + 1) * CALL],
-                            in_=window(rho, j),
+                            out=operands[j][0][:, k * COLS:(k + 1) * COLS].bitcast(FP8X4),
+                            scales=operands[j][1][:, k * COLS:(k + 1) * COLS],
+                            in_=window(r + i, j),
                         )
-                pending.append((gi, i, slots))
-                if (gi, i) == W_AFTER:
-                    w_quantise(0, 8)
-                    w_quantise(8, 1)
-                    w_ready = True
-                if w_ready:
-                    for item in pending:
-                        passes(item[0], item[1], item[2])
-                    pending = []
+                waiting.append((group, i, operands))
+                if (group, i) == WEIGHTS_AFTER:
+                    quantise_weights(0, 8)
+                    quantise_weights(8, 1)
+                    weights_ready = True
+                if weights_ready:
+                    for item in waiting:
+                        multiply(item[0], item[1], item[2])
+                    waiting = []

@@ -15,24 +15,22 @@ IMAGES, CHANNELS, WIDTH, OUT_CH = 4, 512, 34, 128
 OUT_WIDTH = WIDTH - 2
 TAPS = 9
 PACK = 4
-STRIPS = 2 * IMAGES
-STRIP_ROWS = 16
+STRIPS = 8
 LANES = STRIPS * PACK
-IMAGE_LANES = 2 * PACK
 PAIR = 2 * WIDTH
 RUN = 4
 COLS = OUT_WIDTH * STRIPS
 FLOPS = 2 * OUT_CH * CHANNELS * TAPS * IMAGES * OUT_WIDTH * OUT_WIDTH
 
-CHUNKS = ((0, 2), (2, 3), (3, 5), (5, 9))
-HEAD_PAIRS = CHUNKS[0][1]
-HEAD_IMAGES = (2, 3, 0, 1)
-GROUPS = tuple((r, r + 1) for r in range(0, STRIP_ROWS - 2, 2)) + ((STRIP_ROWS - 2,), (STRIP_ROWS - 1,))
-WEIGHTS_AFTER = (3, 0)
-SLOTS = 40
-REGROUP_AFTER_GROUP = {0: (6,), 2: (7,), 3: (8,)}
+BLOCKS = ((0, 0, 2), (0, 16, 2), (1, 0, 4), (2, 0, 4), (3, 0, 2), (3, 16, 2))
+GROUPS = tuple((b, (r, r + 1)) for b in range(len(BLOCKS) - 1) for r in range(0, BLOCKS[b][2], 2)) + (
+    (len(BLOCKS) - 1, (0,)), (len(BLOCKS) - 1, (1,)))
+WEIGHTS_AFTER = (3, 1)
+SLOTS = 36
+LEAD = 24
 TAPS_PER_BANK = 2
 WEIGHT_BANKS = 5
+SPLIT = 36
 
 
 def tile_sparseconv2d_kernel(tc, x, weight, bias, out):
@@ -57,53 +55,38 @@ def tile_sparseconv2d_kernel(tc, x, weight, bias, out):
         nc.scalar.activation(out=warm[:, 1:2], in_=warm[:, 0:1], func=IDENTITY)
 
         staged = []
-        for chunk, (first_pair, end_pair) in enumerate(CHUNKS):
-            rows = 2 * (end_pair - first_pair)
-            pitch = -(-rows * WIDTH // 16) * 16
-            lanes = keep.tile([P, LANES, pitch], BF16, name="staged%d" % chunk)
+        for block, (n, row0, strip_rows) in enumerate(BLOCKS):
+            rows = STRIPS * strip_rows + 2
+            pitch = rows * WIDTH if rows == WIDTH else -(-rows * WIDTH // 16) * 16
+            lanes = keep.tile([P, PACK, pitch], BF16, name="staged%d" % block)
             staged.append(lanes)
-            for strip in [2 * n + h for n in (HEAD_IMAGES if chunk == 0 else range(IMAGES)) for h in range(2)]:
-                n, h = strip // 2, strip % 2
-                row0 = STRIP_ROWS * h + 2 * first_pair
-                nc.sync.dma_start(
-                    out=lanes[:, strip * PACK:(strip + 1) * PACK, 0:rows * WIDTH],
-                    in_=x[n, :, row0:row0 + rows, :].rearrange("(p t) r u -> p t (r u)", t=PACK),
-                )
-            if chunk == 0:
+            nc.sync.dma_start(
+                out=lanes[:, :, 0:rows * WIDTH],
+                in_=x[n, :, row0:row0 + rows, :].rearrange("(p t) r u -> p t (r u)", t=PACK),
+            )
+            if block == 1:
                 nc.sync.dma_start(out=weight_rows[:], in_=weight)
         nc.sync.dma_start(out=bias_col[:], in_=bias)
 
         spread = {}
 
-        def regroup(chunk, target, position0, positions, lane0, lanes, engine_copy):
-            source = staged[chunk][:, lane0:lane0 + lanes, position0:position0 + positions]
+        def regroup(block, pair, low, high, engine_copy):
+            if (block, pair) not in spread:
+                spread[block, pair] = keep.tile([P, PAIR * LANES], BF16, name="spread%d_%d" % (block, pair), align_bytes=64)
+            n, row0, strip_rows = BLOCKS[block]
+            rows = STRIPS * strip_rows + 2
+            step = strip_rows // 2
+            by_pair = staged[block][:, :, 0:rows * WIDTH].rearrange("p t (m u) -> p t m u", u=PAIR)
             engine_copy(
-                out=target.rearrange("p (b i m g) -> p m b g i", i=RUN, m=LANES // lanes, g=lanes)[:, lane0 // lanes],
-                in_=source.rearrange("p g (b i) -> p b g i", i=RUN),
+                out=spread[block, pair][:, low * LANES:high * LANES].rearrange(
+                    "p (b i m t) -> p b m t i", i=RUN, m=STRIPS, t=PACK),
+                in_=by_pair[:, :, pair:pair + (STRIPS - 1) * step + 1:step, low:high].rearrange(
+                    "p t m (b i) -> p b m t i", i=RUN),
             )
 
-        def new_pair(pair):
-            spread[pair] = keep.tile([P, PAIR * LANES], BF16, name="spread%d" % pair, align_bytes=64)
-            chunk = [k for k, (first, end) in enumerate(CHUNKS) if first <= pair < end][0]
-            return chunk, (pair - CHUNKS[chunk][0]) * PAIR
-
-        def regroup_pair(pair):
-            chunk, position0 = new_pair(pair)
-            regroup(chunk, spread[pair][:], position0, PAIR, 0, LANES, nc.scalar.copy)
-
-        def regroup_pair_by_image(pair):
-            chunk, position0 = new_pair(pair)
-            for n in range(IMAGES):
-                regroup(chunk, spread[pair][:], position0, PAIR, n * IMAGE_LANES, IMAGE_LANES, nc.scalar.copy)
-
-        head = keep.tile([P, HEAD_PAIRS * PAIR * LANES], BF16, name="head", align_bytes=64)
-
-        def window(row, j):
-            if row < 2 * HEAD_PAIRS:
-                start = (row * WIDTH + j) * LANES
-                return head[:, start:start + COLS * PACK]
+        def window(block, row, j):
             start = ((row % 2) * WIDTH + j) * LANES
-            return spread[row // 2][:, start:start + COLS * PACK]
+            return spread[block, row // 2][:, start:start + COLS * PACK]
 
         grouped = keep.tile([P, TAPS, OUT_CH, PACK], BF16, name="grouped", align_bytes=64)
         weight_codes = keep.tile([P, TAPS * OUT_CH], U32, name="weight_codes", align_bytes=64)
@@ -134,30 +117,28 @@ def tile_sparseconv2d_kernel(tc, x, weight, bias, out):
                 in_=grouped[:, tap0:tap0 + taps, :, :].rearrange("p k o t -> p (k o t)"),
             )
 
-        head_positions = HEAD_PAIRS * PAIR
-        regroup(0, head[:], 0, head_positions, 2 * IMAGE_LANES, IMAGE_LANES, nc.scalar.copy)
-        regroup(0, head[:], 0, head_positions, 3 * IMAGE_LANES, IMAGE_LANES, nc.scalar.copy)
-        regroup(0, head[:, 0:PAIR * LANES], 0, PAIR, 0, IMAGE_LANES, nc.vector.tensor_copy)
-        regroup(0, head[:, 0:PAIR * LANES], 0, PAIR, IMAGE_LANES, IMAGE_LANES, nc.vector.tensor_copy)
-        regroup(0, head[:, PAIR * LANES:2 * PAIR * LANES], PAIR, PAIR, 0, 2 * IMAGE_LANES, nc.scalar.copy)
+        regroup(0, 0, 0, SPLIT, nc.vector.tensor_copy)
+        regroup(0, 0, SPLIT, PAIR, nc.scalar.copy)
+        regroup(0, 1, 0, SPLIT, nc.scalar.copy)
+        regroup(0, 1, SPLIT, PAIR, nc.scalar.copy)
 
         for bank in range(WEIGHT_BANKS):
             transpose_weights(bank)
 
-        regroup_pair_by_image(2)
+        regroup(1, 0, 0, PAIR, nc.scalar.copy)
+        regroup(1, 1, 0, PAIR, nc.scalar.copy)
+        regroup(2, 0, 0, PAIR, nc.scalar.copy)
         group_weights(0)
         group_weights(1)
+        regroup(2, 1, 0, PAIR, nc.scalar.copy)
         group_weights(2)
-        regroup_pair(3)
         group_weights(3)
         group_weights(4)
-        regroup_pair(4)
-        regroup_pair(5)
 
         sums = {}
 
         def multiply(group, i, operands):
-            width = len(GROUPS[group]) * COLS
+            width = len(GROUPS[group][1]) * COLS
             if i == 0:
                 sums[group] = sums_pool.tile([P, 2 * COLS], F32, name="sums")
             for j in range(3):
@@ -176,7 +157,8 @@ def tile_sparseconv2d_kernel(tc, x, weight, bias, out):
                 finish(group)
 
         def finish(group):
-            rows = GROUPS[group]
+            block, rows = GROUPS[group]
+            n, row0, strip_rows = BLOCKS[block]
             width = len(rows) * COLS
             result = result_pool.tile([P, 2 * COLS], F32, name="result")
             nc.scalar.activation(
@@ -185,38 +167,45 @@ def tile_sparseconv2d_kernel(tc, x, weight, bias, out):
                 func=IDENTITY,
                 bias=bias_col[:, 0:1],
             )
-            by_half = result[:, 0:width].rearrange("o (n h q) -> o n h q", n=IMAGES, h=2)
-            for h in range(2):
-                row0 = STRIP_ROWS * h + rows[0]
-                nc.sync.dma_start(
-                    out=out[:, :, row0:row0 + len(rows), :].rearrange("n o r u -> o n (r u)"),
-                    in_=by_half[:, :, h, :],
-                )
-            for pair in REGROUP_AFTER_GROUP.get(group, ()):
-                regroup_pair(pair)
+            by_strip = out[n, :, row0:row0 + STRIPS * strip_rows, :].rearrange("o (s r) u -> o s r u", r=strip_rows)
+            nc.sync.dma_start(
+                out=by_strip[:, :, rows[0]:rows[0] + len(rows), :].rearrange("o s r u -> o s (r u)"),
+                in_=result[:, 0:width].rearrange("o (s q) -> o s q", s=STRIPS),
+            )
+
+        calls = [(group, i, k, j) for group in range(len(GROUPS)) for i in range(3)
+                 for k in range(len(GROUPS[group][1])) for j in range(3)]
+        first_use = {}
+        for index, (group, i, k, j) in enumerate(calls):
+            block, rows = GROUPS[group]
+            first_use.setdefault((block, (rows[k] + i) // 2), index)
 
         waiting = []
         weights_ready = False
-        for group, rows in enumerate(GROUPS):
-            for i in range(3):
-                operands = []
-                for j in range(3):
-                    codes = slots_pool.tile([P, 2 * COLS], U32, name="codes", align_bytes=64)
-                    scales = slots_pool.tile([P, 2 * COLS], U8, name="scales", align_bytes=64)
-                    operands.append((codes, scales))
-                for k, r in enumerate(rows):
-                    for j in range(3):
-                        nc.vector.quantize_mx(
-                            out=operands[j][0][:, k * COLS:(k + 1) * COLS].bitcast(FP8X4),
-                            scales=operands[j][1][:, k * COLS:(k + 1) * COLS],
-                            in_=window(r + i, j),
-                        )
+        operands = []
+        for index, (group, i, k, j) in enumerate(calls):
+            for key, use in first_use.items():
+                if key not in spread and use <= index + LEAD:
+                    regroup(key[0], key[1], 0, PAIR, nc.scalar.copy)
+            block, rows = GROUPS[group]
+            if k == 0:
+                codes = slots_pool.tile([P, 2 * COLS], U32, name="codes", align_bytes=64)
+                scales = slots_pool.tile([P, 2 * COLS], U8, name="scales", align_bytes=64)
+                operands.append((codes, scales))
+            nc.vector.quantize_mx(
+                out=operands[j][0][:, k * COLS:(k + 1) * COLS].bitcast(FP8X4),
+                scales=operands[j][1][:, k * COLS:(k + 1) * COLS],
+                in_=window(block, rows[k] + i, j),
+            )
+            if j == 2 and k == len(rows) - 1:
                 waiting.append((group, i, operands))
+                operands = []
                 if (group, i) == WEIGHTS_AFTER:
                     quantise_weights(0, 8)
                     quantise_weights(8, 1)
                     weights_ready = True
-                if weights_ready:
-                    for item in waiting:
-                        multiply(item[0], item[1], item[2])
-                    waiting = []
+                for item in range(2 if weights_ready else 0):
+                    if waiting:
+                        multiply(*waiting.pop(0))
+        for item in waiting:
+            multiply(*item)

@@ -15,32 +15,30 @@ IMAGES, CHANNELS, WIDTH, OUT_CH = 4, 512, 34, 128
 OUT_WIDTH = WIDTH - 2
 TAPS = 9
 PACK = 4
-STRIPS = 8
-LANES = STRIPS * PACK
-PAIR = 2 * WIDTH
-RUN = 4
-COLS = OUT_WIDTH * STRIPS
+BANK = 512
 FLOPS = 2 * OUT_CH * CHANNELS * TAPS * IMAGES * OUT_WIDTH * OUT_WIDTH
 
-BLOCKS = ((0, 0, 2), (0, 16, 2), (1, 0, 4), (2, 0, 4), (3, 0, 2), (3, 16, 2))
-GROUPS = tuple((b, (r, r + 1)) for b in range(len(BLOCKS) - 1) for r in range(0, BLOCKS[b][2], 2)) + (
-    (len(BLOCKS) - 1, (0,)), (len(BLOCKS) - 1, (1,)))
-WEIGHTS_AFTER = (3, 1)
-SLOTS = 36
-LEAD = 24
+SECTIONS = ((0, 0, 2, 8), (0, 16, 2, 8), (1, 0, 4, 8), (2, 0, 1, 32), (3, 0, 1, 16), (3, 16, 1, 8), (3, 24, 1, 8))
+SETS = tuple((c, rows) for c in range(len(SECTIONS))
+             for rows in (((0, 1), (2, 3))[:SECTIONS[c][2] // 2] if SECTIONS[c][2] > 1 else ((0,),)))
+WEIGHTS_AFTER = (2, 2)
+SLOTS = 34
+WIDE_SLOTS = 4
+LEAD = 30
 TAPS_PER_BANK = 2
 WEIGHT_BANKS = 5
-SPLIT = 36
 
 
 def tile_sparseconv2d_kernel(tc, x, weight, bias, out):
     nc = tc.nc
     with ExitStack() as ctx:
         keep = ctx.enter_context(tc.tile_pool(name="keep", bufs=1))
+        parts_pool = ctx.enter_context(tc.tile_pool(name="parts", bufs=7))
+        halves_pool = ctx.enter_context(tc.tile_pool(name="halves", bufs=2))
         slots_pool = ctx.enter_context(tc.tile_pool(name="slots", bufs=SLOTS))
-        result_pool = ctx.enter_context(tc.tile_pool(name="result", bufs=3))
-        sums_pool = ctx.enter_context(tc.psum_pool(name="sums", bufs=3))
-        weight_psum = ctx.enter_context(tc.psum_pool(name="weight_psum", bufs=WEIGHT_BANKS))
+        wide_pool = ctx.enter_context(tc.tile_pool(name="wide", bufs=WIDE_SLOTS))
+        result_pool = ctx.enter_context(tc.tile_pool(name="result", bufs=2))
+        psum = ctx.enter_context(tc.psum_pool(name="psum", bufs=8))
 
         identity = keep.tile([P, P], BF16, name="identity")
         make_identity(nc, identity[:])
@@ -54,39 +52,78 @@ def tile_sparseconv2d_kernel(tc, x, weight, bias, out):
         nc.vector.memset(warm[:, 0:1], 0.0)
         nc.scalar.activation(out=warm[:, 1:2], in_=warm[:, 0:1], func=IDENTITY)
 
-        staged = []
-        for block, (n, row0, strip_rows) in enumerate(BLOCKS):
-            rows = STRIPS * strip_rows + 2
+        staged = {}
+
+        def load(section):
+            n, row0, strip_rows, strips = SECTIONS[section]
+            rows = strips * strip_rows + 2
             pitch = rows * WIDTH if rows == WIDTH else -(-rows * WIDTH // 16) * 16
-            lanes = keep.tile([P, PACK, pitch], BF16, name="staged%d" % block)
-            staged.append(lanes)
+            if pitch == 624:
+                staged[section] = halves_pool.tile([P, PACK, pitch], BF16, name="half")
+            else:
+                staged[section] = keep.tile([P, PACK, pitch], BF16, name="staged%d" % section)
             nc.sync.dma_start(
-                out=lanes[:, :, 0:rows * WIDTH],
+                out=staged[section][:, :, 0:rows * WIDTH],
                 in_=x[n, :, row0:row0 + rows, :].rearrange("(p t) r u -> p t (r u)", t=PACK),
             )
-            if block == 1:
-                nc.sync.dma_start(out=weight_rows[:], in_=weight)
-        nc.sync.dma_start(out=bias_col[:], in_=bias)
 
         spread = {}
 
-        def regroup(block, pair, low, high, engine_copy):
-            if (block, pair) not in spread:
-                spread[block, pair] = keep.tile([P, PAIR * LANES], BF16, name="spread%d_%d" % (block, pair), align_bytes=64)
-            n, row0, strip_rows = BLOCKS[block]
-            rows = STRIPS * strip_rows + 2
-            step = strip_rows // 2
-            by_pair = staged[block][:, :, 0:rows * WIDTH].rearrange("p t (m u) -> p t m u", u=PAIR)
+        def part_rows(section):
+            return min(2, SECTIONS[section][2])
+
+        def parts_apart(section):
+            return SECTIONS[section][2] // part_rows(section)
+
+        def new_part(section, part):
+            values = part_rows(section) * WIDTH * SECTIONS[section][3] * PACK
+            if SECTIONS[section][3] == 32:
+                spread[section, part] = keep.tile([P, values], BF16, name="spread%d" % part, align_bytes=64)
+            else:
+                spread[section, part] = parts_pool.tile([P, values], BF16, name="part", align_bytes=64)
+
+        def regroup(section, part, low, high, strip0, strip1, engine_copy):
+            strips = SECTIONS[section][3]
+            if (section, part) not in spread:
+                new_part(section, part)
+            run = 4 if (high - low) % 4 == 0 else 2
+            length = part_rows(section) * WIDTH
+            apart = parts_apart(section)
+            rows = strips * SECTIONS[section][2] + 2
+            by_part = staged[section][:, :, 0:rows * WIDTH].rearrange("p t (m u) -> p t m u", u=length)
+            first = part + strip0 * apart
             engine_copy(
-                out=spread[block, pair][:, low * LANES:high * LANES].rearrange(
-                    "p (b i m t) -> p b m t i", i=RUN, m=STRIPS, t=PACK),
-                in_=by_pair[:, :, pair:pair + (STRIPS - 1) * step + 1:step, low:high].rearrange(
-                    "p t m (b i) -> p b m t i", i=RUN),
+                out=spread[section, part][:, low * strips * PACK:high * strips * PACK].rearrange(
+                    "p (b i m t) -> p b m t i", i=run, m=strips, t=PACK)[:, :, strip0:strip1],
+                in_=by_part[:, :, first:first + (strip1 - strip0 - 1) * apart + 1:apart, low:high].rearrange(
+                    "p t m (b i) -> p b m t i", i=run),
             )
 
-        def window(block, row, j):
-            start = ((row % 2) * WIDTH + j) * LANES
-            return spread[block, row // 2][:, start:start + COLS * PACK]
+        def regroup_part(section, part):
+            length = part_rows(section) * WIDTH
+            strips = SECTIONS[section][3]
+            regroup(section, part, 0, length // 4 * 4, 0, strips, nc.scalar.copy)
+            if length % 4:
+                regroup(section, part, length // 4 * 4, length, 0, strips, nc.scalar.copy)
+
+        def shift(section, part, low, high):
+            apart = parts_apart(section)
+            if (section, part) not in spread:
+                new_part(section, part)
+            left = part // apart * PACK
+            lanes = SECTIONS[section][3] * PACK
+            nc.sync.dma_start(out=spread[section, part][:, low * lanes:high * lanes - left],
+                              in_=spread[section, part % apart][:, low * lanes + left:high * lanes])
+
+        def last_strips(section, part, low, high):
+            strips = SECTIONS[section][3]
+            regroup(section, part, low, high, strips - part // parts_apart(section), strips, nc.scalar.copy)
+
+        def window(section, row, j):
+            lanes = SECTIONS[section][3] * PACK
+            rows = part_rows(section)
+            start = ((row % rows) * WIDTH + j) * lanes
+            return spread[section, row // rows][:, start:start + OUT_WIDTH * lanes]
 
         grouped = keep.tile([P, TAPS, OUT_CH, PACK], BF16, name="grouped", align_bytes=64)
         weight_codes = keep.tile([P, TAPS * OUT_CH], U32, name="weight_codes", align_bytes=64)
@@ -96,7 +133,7 @@ def tile_sparseconv2d_kernel(tc, x, weight, bias, out):
 
         def transpose_weights(bank):
             tap0 = TAPS_PER_BANK * bank
-            turned = weight_psum.tile([P, TAPS_PER_BANK * PACK, OUT_CH], BF16, name="turned")
+            turned = psum.tile([P, TAPS_PER_BANK * PACK, OUT_CH], BF16, name="bank")
             banks.append(turned)
             for k in range(min(TAPS_PER_BANK, TAPS - tap0)):
                 for t in range(PACK):
@@ -117,90 +154,131 @@ def tile_sparseconv2d_kernel(tc, x, weight, bias, out):
                 in_=grouped[:, tap0:tap0 + taps, :, :].rearrange("p k o t -> p (k o t)"),
             )
 
-        regroup(0, 0, 0, SPLIT, nc.vector.tensor_copy)
-        regroup(0, 0, SPLIT, PAIR, nc.scalar.copy)
-        regroup(0, 1, 0, SPLIT, nc.scalar.copy)
-        regroup(0, 1, SPLIT, PAIR, nc.scalar.copy)
+        load(0)
+        load(1)
+        nc.sync.dma_start(out=weight_rows[:], in_=weight)
+        load(2)
+        nc.sync.dma_start(out=bias_col[:], in_=bias)
+
+        regroup(0, 0, 0, 2 * WIDTH, 0, 8, nc.vector.tensor_copy)
+        regroup(0, 1, 0, 36, 0, 8, nc.scalar.copy)
+        regroup(0, 1, 36, 68, 0, 8, nc.scalar.copy)
 
         for bank in range(WEIGHT_BANKS):
             transpose_weights(bank)
 
-        regroup(1, 0, 0, PAIR, nc.scalar.copy)
-        regroup(1, 1, 0, PAIR, nc.scalar.copy)
-        regroup(2, 0, 0, PAIR, nc.scalar.copy)
+        regroup(1, 0, 0, 36, 0, 8, nc.scalar.copy)
+        shift(1, 1, 0, 36)
+        load(3)
+        regroup(1, 0, 36, 68, 0, 8, nc.scalar.copy)
+        shift(1, 1, 36, 68)
+        regroup(2, 0, 0, 36, 0, 8, nc.scalar.copy)
+        last_strips(1, 1, 0, 36)
         group_weights(0)
         group_weights(1)
-        regroup(2, 1, 0, PAIR, nc.scalar.copy)
+        regroup(2, 0, 36, 68, 0, 8, nc.scalar.copy)
+        last_strips(1, 1, 36, 68)
+        shift(2, 2, 0, 68)
+        for section in range(4, len(SECTIONS)):
+            load(section)
+        regroup_part(2, 1)
         group_weights(2)
         group_weights(3)
         group_weights(4)
+        last_strips(2, 2, 0, 68)
 
         sums = {}
+        results = {}
 
-        def multiply(group, i, operands):
-            width = len(GROUPS[group][1]) * COLS
+        def multiply(index, i, operands):
+            section, rows = SETS[index]
+            width = len(rows) * OUT_WIDTH * SECTIONS[section][3]
+            step = min(width, BANK)
             if i == 0:
-                sums[group] = sums_pool.tile([P, 2 * COLS], F32, name="sums")
+                sums[index] = []
+                for start in range(0, width, step):
+                    acc = psum.tile([P, BANK], F32, name="bank")
+                    sums[index].append(acc)
             for j in range(3):
                 tap = 3 * i + j
                 codes, scales = operands[j]
-                nc.tensor.matmul_mx(
-                    out=sums[group][:, 0:width],
-                    lhsT=weight_codes[:, tap * OUT_CH:(tap + 1) * OUT_CH].bitcast(FP8X4),
-                    lhsT_scale=weight_scales[:, tap * OUT_CH:(tap + 1) * OUT_CH],
-                    rhs=codes[:, 0:width].bitcast(FP8X4),
-                    rhs_scale=scales[:, 0:width],
-                    start=(tap == 0),
-                    stop=(tap == TAPS - 1),
-                )
+                for part, acc in enumerate(sums[index]):
+                    nc.tensor.matmul_mx(
+                        out=acc[:, 0:step],
+                        lhsT=weight_codes[:, tap * OUT_CH:(tap + 1) * OUT_CH].bitcast(FP8X4),
+                        lhsT_scale=weight_scales[:, tap * OUT_CH:(tap + 1) * OUT_CH],
+                        rhs=codes[:, part * step:(part + 1) * step].bitcast(FP8X4),
+                        rhs_scale=scales[:, part * step:(part + 1) * step],
+                        start=(tap == 0),
+                        stop=(tap == TAPS - 1),
+                    )
             if i == 2:
-                finish(group)
+                finish(index)
 
-        def finish(group):
-            block, rows = GROUPS[group]
-            n, row0, strip_rows = BLOCKS[block]
-            width = len(rows) * COLS
-            result = result_pool.tile([P, 2 * COLS], F32, name="result")
-            nc.scalar.activation(
-                out=result[:, 0:width].rearrange("o (s q) -> o s q", s=STRIPS),
-                in_=sums[group][:, 0:width].rearrange("o (q s) -> o s q", s=STRIPS),
-                func=IDENTITY,
-                bias=bias_col[:, 0:1],
-            )
-            by_strip = out[n, :, row0:row0 + STRIPS * strip_rows, :].rearrange("o (s r) u -> o s r u", r=strip_rows)
+        def finish(index):
+            section, rows = SETS[index]
+            n, row0, strip_rows, strips = SECTIONS[section]
+            width = len(rows) * OUT_WIDTH * strips
+            step = min(width, BANK)
+            result = result_pool.tile([P, 2 * BANK], F32, name="result")
+            by_strip = result[:, 0:width].rearrange("o (s q) -> o s q", s=strips)
+            share = step // strips
+            for part, acc in enumerate(sums[index]):
+                nc.scalar.activation(
+                    out=by_strip[:, :, part * share:(part + 1) * share],
+                    in_=acc[:, 0:step].rearrange("o (q s) -> o s q", s=strips),
+                    func=IDENTITY,
+                    bias=bias_col[:, 0:1],
+                )
+            rows_out = out[n, :, row0:row0 + strips * strip_rows, :].rearrange("o (s r) u -> o s r u", r=strip_rows)
             nc.sync.dma_start(
-                out=by_strip[:, :, rows[0]:rows[0] + len(rows), :].rearrange("o s r u -> o s (r u)"),
-                in_=result[:, 0:width].rearrange("o (s q) -> o s q", s=STRIPS),
+                out=rows_out[:, :, rows[0]:rows[0] + len(rows), :].rearrange("o s r u -> o s (r u)"),
+                in_=by_strip,
             )
 
-        calls = [(group, i, k, j) for group in range(len(GROUPS)) for i in range(3)
-                 for k in range(len(GROUPS[group][1])) for j in range(3)]
+        calls = [(index, i, k, j) for index in range(len(SETS)) for i in range(3)
+                 for k in range(len(SETS[index][1])) for j in range(3)]
         first_use = {}
-        for index, (group, i, k, j) in enumerate(calls):
-            block, rows = GROUPS[group]
-            first_use.setdefault((block, (rows[k] + i) // 2), index)
+        clock = 0
+        starts = []
+        for index, i, k, j in calls:
+            section, rows = SETS[index]
+            first_use.setdefault((section, (rows[k] + i) // part_rows(section)), clock)
+            starts.append(clock)
+            clock += SECTIONS[section][3] // 8
 
+        done = {(2, 2)}
         waiting = []
         weights_ready = False
         operands = []
-        for index, (group, i, k, j) in enumerate(calls):
+        for call, now in zip(calls, starts):
             for key, use in first_use.items():
-                if key not in spread and use <= index + LEAD:
-                    regroup(key[0], key[1], 0, PAIR, nc.scalar.copy)
-            block, rows = GROUPS[group]
+                section, part = key
+                if section > 2 and use <= now + LEAD and key not in spread and part < parts_apart(section):
+                    regroup_part(section, part)
+                    for later in range(parts_apart(section), len([k for k in first_use if k[0] == section])):
+                        shift(section, later, 0, WIDTH)
+                if section > 2 and use <= now + LEAD // 4 and part >= parts_apart(section) and key not in done:
+                    done.add(key)
+                    last_strips(section, part, 0, WIDTH)
+            index, i, k, j = call
+            section, rows = SETS[index]
+            cols = OUT_WIDTH * SECTIONS[section][3]
             if k == 0:
-                codes = slots_pool.tile([P, 2 * COLS], U32, name="codes", align_bytes=64)
-                scales = slots_pool.tile([P, 2 * COLS], U8, name="scales", align_bytes=64)
+                pool = wide_pool if cols > BANK else slots_pool
+                width = 2 * BANK if cols > BANK else BANK
+                codes = pool.tile([P, width], U32, name="codes", align_bytes=64)
+                scales = pool.tile([P, width], U8, name="scales", align_bytes=64)
                 operands.append((codes, scales))
             nc.vector.quantize_mx(
-                out=operands[j][0][:, k * COLS:(k + 1) * COLS].bitcast(FP8X4),
-                scales=operands[j][1][:, k * COLS:(k + 1) * COLS],
-                in_=window(block, rows[k] + i, j),
+                out=operands[j][0][:, k * cols:(k + 1) * cols].bitcast(FP8X4),
+                scales=operands[j][1][:, k * cols:(k + 1) * cols],
+                in_=window(section, rows[k] + i, j),
             )
             if j == 2 and k == len(rows) - 1:
-                waiting.append((group, i, operands))
+                waiting.append((index, i, operands))
                 operands = []
-                if (group, i) == WEIGHTS_AFTER:
+                if (index, i) == WEIGHTS_AFTER:
                     quantise_weights(0, 8)
                     quantise_weights(8, 1)
                     weights_ready = True

@@ -18,13 +18,12 @@ PACK = 4
 BANK = 512
 FLOPS = 2 * OUT_CH * CHANNELS * TAPS * IMAGES * OUT_WIDTH * OUT_WIDTH
 
-SECTIONS = ((0, 0, 2, 8), (0, 16, 2, 8), (1, 0, 4, 8), (2, 0, 1, 32), (3, 0, 1, 16), (3, 16, 1, 8), (3, 24, 1, 8))
+SECTIONS = ((0, 0, 2, 8), (0, 16, 2, 8), (1, 0, 4, 8), (2, 0, 4, 8), (3, 0, 2, 8), (3, 16, 1, 8), (3, 24, 1, 8))
 SETS = tuple((c, rows) for c in range(len(SECTIONS))
              for rows in (((0, 1), (2, 3))[:SECTIONS[c][2] // 2] if SECTIONS[c][2] > 1 else ((0,),)))
 WEIGHTS_AFTER = (2, 2)
-SLOTS = 34
-WIDE_SLOTS = 4
-LEAD = 30
+SLOTS = 36
+LEAD = 24
 TAPS_PER_BANK = 2
 WEIGHT_BANKS = 5
 
@@ -33,10 +32,9 @@ def tile_sparseconv2d_kernel(tc, x, weight, bias, out):
     nc = tc.nc
     with ExitStack() as ctx:
         keep = ctx.enter_context(tc.tile_pool(name="keep", bufs=1))
-        parts_pool = ctx.enter_context(tc.tile_pool(name="parts", bufs=7))
+        parts_pool = ctx.enter_context(tc.tile_pool(name="parts", bufs=10))
         halves_pool = ctx.enter_context(tc.tile_pool(name="halves", bufs=2))
         slots_pool = ctx.enter_context(tc.tile_pool(name="slots", bufs=SLOTS))
-        wide_pool = ctx.enter_context(tc.tile_pool(name="wide", bufs=WIDE_SLOTS))
         result_pool = ctx.enter_context(tc.tile_pool(name="result", bufs=2))
         psum = ctx.enter_context(tc.psum_pool(name="psum", bufs=8))
 
@@ -77,10 +75,7 @@ def tile_sparseconv2d_kernel(tc, x, weight, bias, out):
 
         def new_part(section, part):
             values = part_rows(section) * WIDTH * SECTIONS[section][3] * PACK
-            if SECTIONS[section][3] == 32:
-                spread[section, part] = keep.tile([P, values], BF16, name="spread%d" % part, align_bytes=64)
-            else:
-                spread[section, part] = parts_pool.tile([P, values], BF16, name="part", align_bytes=64)
+            spread[section, part] = parts_pool.tile([P, values], BF16, name="part", align_bytes=64)
 
         def regroup(section, part, low, high, strip0, strip1, engine_copy):
             strips = SECTIONS[section][3]
@@ -99,25 +94,27 @@ def tile_sparseconv2d_kernel(tc, x, weight, bias, out):
                     "p t m (b i) -> p b m t i", i=run),
             )
 
-        def regroup_part(section, part):
+        def make_part(section, part):
+            if part >= parts_apart(section):
+                shift(section, part)
+                last_strips(section, part)
+                return
             length = part_rows(section) * WIDTH
             strips = SECTIONS[section][3]
             regroup(section, part, 0, length // 4 * 4, 0, strips, nc.scalar.copy)
             if length % 4:
                 regroup(section, part, length // 4 * 4, length, 0, strips, nc.scalar.copy)
 
-        def shift(section, part, low, high):
+        def shift(section, part):
             apart = parts_apart(section)
-            if (section, part) not in spread:
-                new_part(section, part)
+            new_part(section, part)
             left = part // apart * PACK
-            lanes = SECTIONS[section][3] * PACK
-            nc.sync.dma_start(out=spread[section, part][:, low * lanes:high * lanes - left],
-                              in_=spread[section, part % apart][:, low * lanes + left:high * lanes])
+            values = part_rows(section) * WIDTH * SECTIONS[section][3] * PACK
+            nc.scalar.copy(out=spread[section, part][:, 0:values - left], in_=spread[section, part % apart][:, left:values])
 
-        def last_strips(section, part, low, high):
+        def last_strips(section, part):
             strips = SECTIONS[section][3]
-            regroup(section, part, low, high, strips - part // parts_apart(section), strips, nc.scalar.copy)
+            regroup(section, part, 0, part_rows(section) * WIDTH, strips - part // parts_apart(section), strips, nc.scalar.copy)
 
         def window(section, row, j):
             lanes = SECTIONS[section][3] * PACK
@@ -159,6 +156,8 @@ def tile_sparseconv2d_kernel(tc, x, weight, bias, out):
         nc.sync.dma_start(out=weight_rows[:], in_=weight)
         load(2)
         nc.sync.dma_start(out=bias_col[:], in_=bias)
+        for section in range(3, len(SECTIONS)):
+            load(section)
 
         regroup(0, 0, 0, 2 * WIDTH, 0, 8, nc.vector.tensor_copy)
         regroup(0, 1, 0, 36, 0, 8, nc.scalar.copy)
@@ -167,25 +166,16 @@ def tile_sparseconv2d_kernel(tc, x, weight, bias, out):
         for bank in range(WEIGHT_BANKS):
             transpose_weights(bank)
 
-        regroup(1, 0, 0, 36, 0, 8, nc.scalar.copy)
-        shift(1, 1, 0, 36)
-        load(3)
-        regroup(1, 0, 36, 68, 0, 8, nc.scalar.copy)
-        shift(1, 1, 36, 68)
-        regroup(2, 0, 0, 36, 0, 8, nc.scalar.copy)
-        last_strips(1, 1, 0, 36)
+        make_part(1, 0)
+        make_part(1, 1)
+        make_part(2, 0)
         group_weights(0)
+        make_part(2, 1)
         group_weights(1)
-        regroup(2, 0, 36, 68, 0, 8, nc.scalar.copy)
-        last_strips(1, 1, 36, 68)
-        shift(2, 2, 0, 68)
-        for section in range(4, len(SECTIONS)):
-            load(section)
-        regroup_part(2, 1)
         group_weights(2)
         group_weights(3)
         group_weights(4)
-        last_strips(2, 2, 0, 68)
+        make_part(2, 2)
 
         sums = {}
         results = {}
@@ -247,28 +237,19 @@ def tile_sparseconv2d_kernel(tc, x, weight, bias, out):
             starts.append(clock)
             clock += SECTIONS[section][3] // 8
 
-        done = {(2, 2)}
         waiting = []
         weights_ready = False
         operands = []
         for call, now in zip(calls, starts):
             for key, use in first_use.items():
-                section, part = key
-                if section > 2 and use <= now + LEAD and key not in spread and part < parts_apart(section):
-                    regroup_part(section, part)
-                    for later in range(parts_apart(section), len([k for k in first_use if k[0] == section])):
-                        shift(section, later, 0, WIDTH)
-                if section > 2 and use <= now + LEAD // 4 and part >= parts_apart(section) and key not in done:
-                    done.add(key)
-                    last_strips(section, part, 0, WIDTH)
+                if use <= now + LEAD and key not in spread:
+                    make_part(*key)
             index, i, k, j = call
             section, rows = SETS[index]
             cols = OUT_WIDTH * SECTIONS[section][3]
             if k == 0:
-                pool = wide_pool if cols > BANK else slots_pool
-                width = 2 * BANK if cols > BANK else BANK
-                codes = pool.tile([P, width], U32, name="codes", align_bytes=64)
-                scales = pool.tile([P, width], U8, name="scales", align_bytes=64)
+                codes = slots_pool.tile([P, BANK], U32, name="codes", align_bytes=64)
+                scales = slots_pool.tile([P, BANK], U8, name="scales", align_bytes=64)
                 operands.append((codes, scales))
             nc.vector.quantize_mx(
                 out=operands[j][0][:, k * cols:(k + 1) * cols].bitcast(FP8X4),

@@ -159,7 +159,9 @@ def tile_sparseconv2d_kernel(tc, x, weight, bias, out):
         for section in range(3, len(SECTIONS)):
             load(section)
 
-        regroup(0, 0, 0, 2 * WIDTH, 0, 8, nc.vector.tensor_copy)
+        regroup(0, 0, 0, 32, 0, 8, nc.vector.tensor_copy)
+        regroup(0, 0, 32, 64, 0, 8, nc.vector.tensor_copy)
+        regroup(0, 0, 64, 68, 0, 8, nc.vector.tensor_copy)
         regroup(0, 1, 0, 36, 0, 8, nc.scalar.copy)
         regroup(0, 1, 36, 68, 0, 8, nc.scalar.copy)
 

@@ -60,10 +60,16 @@ def tile_sparseconv2d_kernel(tc, x, weight, bias, out):
                 staged[section] = halves_pool.tile([P, PACK, pitch], BF16, name="half")
             else:
                 staged[section] = keep.tile([P, PACK, pitch], BF16, name="staged%d" % section)
-            nc.sync.dma_start(
-                out=staged[section][:, :, 0:rows * WIDTH],
-                in_=x[n, :, row0:row0 + rows, :].rearrange("(p t) r u -> p t (r u)", t=PACK),
-            )
+            if rows == WIDTH:
+                nc.sync.dma_start(
+                    out=staged[section][:].rearrange("p t u -> p (t u)"),
+                    in_=x[n].rearrange("(p t) r u -> p (t r u)", t=PACK),
+                )
+            else:
+                nc.sync.dma_start(
+                    out=staged[section][:, :, 0:rows * WIDTH],
+                    in_=x[n, :, row0:row0 + rows, :].rearrange("(p t) r u -> p t (r u)", t=PACK),
+                )
 
         spread = {}
 

@@ -19,10 +19,11 @@ BANK = 512
 FLOPS = 2 * OUT_CH * CHANNELS * TAPS * IMAGES * OUT_WIDTH * OUT_WIDTH
 
 SECTIONS = ((0, 0, 2, 8), (0, 16, 2, 8), (1, 0, 4, 8), (2, 0, 4, 8), (3, 0, 2, 8), (3, 16, 1, 8), (3, 24, 1, 8))
+PIECES = {0: 2}
 SETS = tuple((c, rows) for c in range(len(SECTIONS))
              for rows in (((0, 1), (2, 3))[:SECTIONS[c][2] // 2] if SECTIONS[c][2] > 1 else ((0,),)))
-WEIGHTS_AFTER = (2, 2)
-SLOTS = 36
+WEIGHTS_AFTER = (3, 0)
+SLOTS = 42
 LEAD = 24
 TAPS_PER_BANK = 2
 WEIGHT_BANKS = 5
@@ -33,9 +34,8 @@ def tile_sparseconv2d_kernel(tc, x, weight, bias, out):
     with ExitStack() as ctx:
         keep = ctx.enter_context(tc.tile_pool(name="keep", bufs=1))
         parts_pool = ctx.enter_context(tc.tile_pool(name="parts", bufs=10))
-        halves_pool = ctx.enter_context(tc.tile_pool(name="halves", bufs=2))
         slots_pool = ctx.enter_context(tc.tile_pool(name="slots", bufs=SLOTS))
-        result_pool = ctx.enter_context(tc.tile_pool(name="result", bufs=2))
+        result_pool = ctx.enter_context(tc.tile_pool(name="result", bufs=4))
         psum = ctx.enter_context(tc.psum_pool(name="psum", bufs=8))
 
         identity = keep.tile([P, P], BF16, name="identity")
@@ -52,22 +52,22 @@ def tile_sparseconv2d_kernel(tc, x, weight, bias, out):
 
         staged = {}
 
-        def load(section):
+        def load(section, piece=0):
             n, row0, strip_rows, strips = SECTIONS[section]
+            strips //= PIECES.get(section, 1)
+            row0 += piece * strips * strip_rows
             rows = strips * strip_rows + 2
             pitch = rows * WIDTH if rows == WIDTH else -(-rows * WIDTH // 16) * 16
-            if pitch == 624:
-                staged[section] = halves_pool.tile([P, PACK, pitch], BF16, name="half")
-            else:
-                staged[section] = keep.tile([P, PACK, pitch], BF16, name="staged%d" % section)
+            lanes = keep.tile([P, PACK, pitch], BF16, name="staged%d_%d" % (section, piece))
+            staged[section, piece] = lanes
             if rows == WIDTH:
                 nc.sync.dma_start(
-                    out=staged[section][:].rearrange("p t u -> p (t u)"),
+                    out=lanes[:].rearrange("p t u -> p (t u)"),
                     in_=x[n].rearrange("(p t) r u -> p (t r u)", t=PACK),
                 )
             else:
                 nc.sync.dma_start(
-                    out=staged[section][:, :, 0:rows * WIDTH],
+                    out=lanes[:, :, 0:rows * WIDTH],
                     in_=x[n, :, row0:row0 + rows, :].rearrange("(p t) r u -> p t (r u)", t=PACK),
                 )
 
@@ -90,9 +90,11 @@ def tile_sparseconv2d_kernel(tc, x, weight, bias, out):
             run = 4 if (high - low) % 4 == 0 else 2
             length = part_rows(section) * WIDTH
             apart = parts_apart(section)
-            rows = strips * SECTIONS[section][2] + 2
-            by_part = staged[section][:, :, 0:rows * WIDTH].rearrange("p t (m u) -> p t m u", u=length)
-            first = part + strip0 * apart
+            piece_strips = strips // PIECES.get(section, 1)
+            piece = strip0 // piece_strips
+            rows = piece_strips * SECTIONS[section][2] + 2
+            by_part = staged[section, piece][:, :, 0:rows * WIDTH].rearrange("p t (m u) -> p t m u", u=length)
+            first = part + (strip0 - piece * piece_strips) * apart
             engine_copy(
                 out=spread[section, part][:, low * strips * PACK:high * strips * PACK].rearrange(
                     "p (b i m t) -> p b m t i", i=run, m=strips, t=PACK)[:, :, strip0:strip1],
@@ -157,19 +159,19 @@ def tile_sparseconv2d_kernel(tc, x, weight, bias, out):
                 in_=grouped[:, tap0:tap0 + taps, :, :].rearrange("p k o t -> p (k o t)"),
             )
 
-        load(0)
+        load(0, 0)
+        load(0, 1)
         load(1)
-        nc.sync.dma_start(out=weight_rows[:], in_=weight)
         load(2)
+        nc.sync.dma_start(out=weight_rows[:], in_=weight)
         nc.sync.dma_start(out=bias_col[:], in_=bias)
         for section in range(3, len(SECTIONS)):
             load(section)
 
-        regroup(0, 0, 0, 32, 0, 8, nc.vector.tensor_copy)
-        regroup(0, 0, 32, 64, 0, 8, nc.vector.tensor_copy)
-        regroup(0, 0, 64, 68, 0, 8, nc.vector.tensor_copy)
-        regroup(0, 1, 0, 36, 0, 8, nc.scalar.copy)
-        regroup(0, 1, 36, 68, 0, 8, nc.scalar.copy)
+        for strip in (0, 4):
+            regroup(0, 0, 0, 64, strip, strip + 4, nc.vector.tensor_copy)
+            regroup(0, 0, 64, 68, strip, strip + 4, nc.vector.tensor_copy)
+            regroup(0, 1, 0, 68, strip, strip + 4, nc.scalar.copy)
 
         for bank in range(WEIGHT_BANKS):
             transpose_weights(bank)
@@ -177,13 +179,10 @@ def tile_sparseconv2d_kernel(tc, x, weight, bias, out):
         make_part(1, 0)
         make_part(1, 1)
         make_part(2, 0)
-        group_weights(0)
         make_part(2, 1)
-        group_weights(1)
-        group_weights(2)
-        group_weights(3)
-        group_weights(4)
         make_part(2, 2)
+        for bank in range(WEIGHT_BANKS):
+            group_weights(bank)
 
         sums = {}
         results = {}
@@ -218,7 +217,7 @@ def tile_sparseconv2d_kernel(tc, x, weight, bias, out):
             n, row0, strip_rows, strips = SECTIONS[section]
             width = len(rows) * OUT_WIDTH * strips
             step = min(width, BANK)
-            result = result_pool.tile([P, 2 * BANK], F32, name="result")
+            result = result_pool.tile([P, BANK], F32, name="result")
             by_strip = result[:, 0:width].rearrange("o (s q) -> o s q", s=strips)
             share = step // strips
             for part, acc in enumerate(sums[index]):

@@ -19,7 +19,7 @@ BANK = 512
 FLOPS = 2 * OUT_CH * CHANNELS * TAPS * IMAGES * OUT_WIDTH * OUT_WIDTH
 
 SECTIONS = ((0, 0, 2, 8), (0, 16, 2, 8), (1, 0, 4, 8), (2, 0, 4, 8), (3, 0, 2, 8), (3, 16, 1, 8), (3, 24, 1, 8))
-PIECES = {0: 2}
+LOAD_ROWS = {0: ((0, 8), (8, 16), (16, 18))}
 SETS = tuple((c, rows) for c in range(len(SECTIONS))
              for rows in (((0, 1), (2, 3))[:SECTIONS[c][2] // 2] if SECTIONS[c][2] > 1 else ((0,),)))
 WEIGHTS_AFTER = (3, 0)
@@ -52,23 +52,24 @@ def tile_sparseconv2d_kernel(tc, x, weight, bias, out):
 
         staged = {}
 
-        def load(section, piece=0):
+        def load(section):
             n, row0, strip_rows, strips = SECTIONS[section]
-            strips //= PIECES.get(section, 1)
-            row0 += piece * strips * strip_rows
             rows = strips * strip_rows + 2
-            pitch = rows * WIDTH if rows == WIDTH else -(-rows * WIDTH // 16) * 16
-            lanes = keep.tile([P, PACK, pitch], BF16, name="staged%d_%d" % (section, piece))
-            staged[section, piece] = lanes
             if rows == WIDTH:
+                lanes = keep.tile([P, PACK, rows * WIDTH], BF16, name="staged%d" % section)
+                staged[section] = [(0, rows, lanes)]
                 nc.sync.dma_start(
                     out=lanes[:].rearrange("p t u -> p (t u)"),
                     in_=x[n].rearrange("(p t) r u -> p (t r u)", t=PACK),
                 )
-            else:
+                return
+            staged[section] = []
+            for low, high in LOAD_ROWS.get(section, ((0, rows),)):
+                lanes = keep.tile([P, PACK, -(-(high - low) * WIDTH // 16) * 16], BF16, name="staged%d_%d" % (section, low))
+                staged[section].append((low, high, lanes))
                 nc.sync.dma_start(
-                    out=lanes[:, :, 0:rows * WIDTH],
-                    in_=x[n, :, row0:row0 + rows, :].rearrange("(p t) r u -> p t (r u)", t=PACK),
+                    out=lanes[:, :, 0:(high - low) * WIDTH],
+                    in_=x[n, :, row0 + low:row0 + high, :].rearrange("(p t) r u -> p t (r u)", t=PACK),
                 )
 
         spread = {}
@@ -90,11 +91,10 @@ def tile_sparseconv2d_kernel(tc, x, weight, bias, out):
             run = 4 if (high - low) % 4 == 0 else 2
             length = part_rows(section) * WIDTH
             apart = parts_apart(section)
-            piece_strips = strips // PIECES.get(section, 1)
-            piece = strip0 // piece_strips
-            rows = piece_strips * SECTIONS[section][2] + 2
-            by_part = staged[section, piece][:, :, 0:rows * WIDTH].rearrange("p t (m u) -> p t m u", u=length)
-            first = part + (strip0 - piece * piece_strips) * apart
+            first = part + strip0 * apart
+            start, end, lanes_in = [load for load in staged[section] if load[0] <= first * part_rows(section) < load[1]][0]
+            by_part = lanes_in[:, :, 0:(end - start) * WIDTH].rearrange("p t (m u) -> p t m u", u=length)
+            first -= start // part_rows(section)
             engine_copy(
                 out=spread[section, part][:, low * strips * PACK:high * strips * PACK].rearrange(
                     "p (b i m t) -> p b m t i", i=run, m=strips, t=PACK)[:, :, strip0:strip1],
@@ -159,8 +159,7 @@ def tile_sparseconv2d_kernel(tc, x, weight, bias, out):
                 in_=grouped[:, tap0:tap0 + taps, :, :].rearrange("p k o t -> p (k o t)"),
             )
 
-        load(0, 0)
-        load(0, 1)
+        load(0)
         load(1)
         load(2)
         nc.sync.dma_start(out=weight_rows[:], in_=weight)
@@ -168,10 +167,12 @@ def tile_sparseconv2d_kernel(tc, x, weight, bias, out):
         for section in range(3, len(SECTIONS)):
             load(section)
 
-        for strip in (0, 4):
-            regroup(0, 0, 0, 64, strip, strip + 4, nc.vector.tensor_copy)
-            regroup(0, 0, 64, 68, strip, strip + 4, nc.vector.tensor_copy)
-            regroup(0, 1, 0, 68, strip, strip + 4, nc.scalar.copy)
+        regroup(0, 0, 0, 64, 0, 4, nc.vector.tensor_copy)
+        regroup(0, 0, 64, 68, 0, 4, nc.vector.tensor_copy)
+        regroup(0, 0, 0, 32, 4, 8, nc.vector.tensor_copy)
+        regroup(0, 0, 32, 36, 4, 8, nc.vector.tensor_copy)
+        regroup(0, 0, 36, 68, 4, 8, nc.scalar.copy)
+        make_part(0, 1)
 
         for bank in range(WEIGHT_BANKS):
             transpose_weights(bank)
@@ -187,10 +188,15 @@ def tile_sparseconv2d_kernel(tc, x, weight, bias, out):
         sums = {}
         results = {}
 
+        def pass_columns(index):
+            section, rows = SETS[index]
+            columns = len(rows) * OUT_WIDTH * SECTIONS[section][3]
+            return columns // 2 if index == len(SETS) - 1 else min(columns, BANK)
+
         def multiply(index, i, operands):
             section, rows = SETS[index]
             width = len(rows) * OUT_WIDTH * SECTIONS[section][3]
-            step = min(width, BANK)
+            step = pass_columns(index)
             if i == 0:
                 sums[index] = []
                 for start in range(0, width, step):
@@ -216,7 +222,7 @@ def tile_sparseconv2d_kernel(tc, x, weight, bias, out):
             section, rows = SETS[index]
             n, row0, strip_rows, strips = SECTIONS[section]
             width = len(rows) * OUT_WIDTH * strips
-            step = min(width, BANK)
+            step = pass_columns(index)
             result = result_pool.tile([P, BANK], F32, name="result")
             by_strip = result[:, 0:width].rearrange("o (s q) -> o s q", s=strips)
             share = step // strips
@@ -258,11 +264,13 @@ def tile_sparseconv2d_kernel(tc, x, weight, bias, out):
                 codes = slots_pool.tile([P, BANK], U32, name="codes", align_bytes=64)
                 scales = slots_pool.tile([P, BANK], U8, name="scales", align_bytes=64)
                 operands.append((codes, scales))
-            nc.vector.quantize_mx(
-                out=operands[j][0][:, k * cols:(k + 1) * cols].bitcast(FP8X4),
-                scales=operands[j][1][:, k * cols:(k + 1) * cols],
-                in_=window(section, rows[k] + i, j),
-            )
+            share = cols // 2 if call == calls[-1] else cols
+            for start in range(0, cols, share):
+                nc.vector.quantize_mx(
+                    out=operands[j][0][:, k * cols + start:k * cols + start + share].bitcast(FP8X4),
+                    scales=operands[j][1][:, k * cols + start:k * cols + start + share],
+                    in_=window(section, rows[k] + i, j)[:, start * PACK:(start + share) * PACK],
+                )
             if j == 2 and k == len(rows) - 1:
                 waiting.append((index, i, operands))
                 operands = []

from contextlib import ExitStack

import concourse.mybir as mybir
from concourse.masks import make_identity

F32 = mybir.dt.float32
BF16 = mybir.dt.bfloat16
U32 = mybir.dt.uint32
U8 = mybir.dt.uint8
FP8X4 = mybir.dt.float8_e4m3fn_x4
IDENTITY = mybir.ActivationFunctionType.Identity

P = 128
IMAGES, CHANNELS, WIDTH, OUT_CH = 4, 512, 34, 128
OUT_WIDTH = WIDTH - 2
TAPS = 9
PACK = 4
BANK = 512
FLOPS = 2 * OUT_CH * CHANNELS * TAPS * IMAGES * OUT_WIDTH * OUT_WIDTH

SECTIONS = ((0, 0, 2, 8), (0, 16, 2, 8), (1, 0, 4, 8), (2, 0, 4, 8), (3, 0, 2, 8), (3, 16, 1, 8), (3, 24, 1, 8))
LOAD_ROWS = {0: ((0, 8), (8, 16), (16, 18))}
SETS = tuple((c, rows) for c in range(len(SECTIONS))
             for rows in (((0, 1), (2, 3))[:SECTIONS[c][2] // 2] if SECTIONS[c][2] > 1 else ((0,),)))
WEIGHTS_AFTER = (3, 0)
SLOTS = 42
LEAD = 24
TAPS_PER_BANK = 2
WEIGHT_BANKS = 5


def tile_sparseconv2d_kernel(tc, x, weight, bias, out):
    nc = tc.nc
    with ExitStack() as ctx:
        keep = ctx.enter_context(tc.tile_pool(name="keep", bufs=1))
        parts_pool = ctx.enter_context(tc.tile_pool(name="parts", bufs=10))
        slots_pool = ctx.enter_context(tc.tile_pool(name="slots", bufs=SLOTS))
        result_pool = ctx.enter_context(tc.tile_pool(name="result", bufs=4))
        psum = ctx.enter_context(tc.psum_pool(name="psum", bufs=8))

        identity = keep.tile([P, P], BF16, name="identity")
        make_identity(nc, identity[:])

        ctx.enter_context(tc.manual_schedule())

        weight_rows = keep.tile([P, CHANNELS * TAPS], BF16, name="weight_rows")
        bias_col = keep.tile([P, 1], BF16, name="bias_col")

        warm = keep.tile([P, 2], F32, name="warm")
        nc.vector.memset(warm[:, 0:1], 0.0)
        nc.scalar.activation(out=warm[:, 1:2], in_=warm[:, 0:1], func=IDENTITY)

        staged = {}

        def load(section):
            n, row0, strip_rows, strips = SECTIONS[section]
            rows = strips * strip_rows + 2
            if rows == WIDTH:
                lanes = keep.tile([P, PACK, rows * WIDTH], BF16, name="staged%d" % section)
                staged[section] = [(0, rows, lanes)]
                nc.sync.dma_start(
                    out=lanes[:].rearrange("p t u -> p (t u)"),
                    in_=x[n].rearrange("(p t) r u -> p (t r u)", t=PACK),
                )
                return
            staged[section] = []
            for low, high in LOAD_ROWS.get(section, ((0, rows),)):
                lanes = keep.tile([P, PACK, -(-(high - low) * WIDTH // 16) * 16], BF16, name="staged%d_%d" % (section, low))
                staged[section].append((low, high, lanes))
                nc.sync.dma_start(
                    out=lanes[:, :, 0:(high - low) * WIDTH],
                    in_=x[n, :, row0 + low:row0 + high, :].rearrange("(p t) r u -> p t (r u)", t=PACK),
                )

        spread = {}

        def part_rows(section):
            return min(2, SECTIONS[section][2])

        def parts_apart(section):
            return SECTIONS[section][2] // part_rows(section)

        def new_part(section, part):
            values = part_rows(section) * WIDTH * SECTIONS[section][3] * PACK
            spread[section, part] = parts_pool.tile([P, values], BF16, name="part", align_bytes=64)

        def regroup(section, part, low, high, strip0, strip1, engine_copy):
            strips = SECTIONS[section][3]
            if (section, part) not in spread:
                new_part(section, part)
            run = 4 if (high - low) % 4 == 0 else 2
            length = part_rows(section) * WIDTH
            apart = parts_apart(section)
            first = part + strip0 * apart
            start, end, lanes_in = [load for load in staged[section] if load[0] <= first * part_rows(section) < load[1]][0]
            by_part = lanes_in[:, :, 0:(end - start) * WIDTH].rearrange("p t (m u) -> p t m u", u=length)
            first -= start // part_rows(section)
            engine_copy(
                out=spread[section, part][:, low * strips * PACK:high * strips * PACK].rearrange(
                    "p (b i m t) -> p b m t i", i=run, m=strips, t=PACK)[:, :, strip0:strip1],
                in_=by_part[:, :, first:first + (strip1 - strip0 - 1) * apart + 1:apart, low:high].rearrange(
                    "p t m (b i) -> p b m t i", i=run),
            )

        def make_part(section, part):
            if part >= parts_apart(section):
                shift(section, part)
                last_strips(section, part)
                return
            length = part_rows(section) * WIDTH
            strips = SECTIONS[section][3]
            regroup(section, part, 0, length // 4 * 4, 0, strips, nc.scalar.copy)
            if length % 4:
                regroup(section, part, length // 4 * 4, length, 0, strips, nc.scalar.copy)

        def shift(section, part):
            apart = parts_apart(section)
            new_part(section, part)
            left = part // apart * PACK
            values = part_rows(section) * WIDTH * SECTIONS[section][3] * PACK
            nc.scalar.copy(out=spread[section, part][:, 0:values - left], in_=spread[section, part % apart][:, left:values])

        def last_strips(section, part):
            strips = SECTIONS[section][3]
            regroup(section, part, 0, part_rows(section) * WIDTH, strips - part // parts_apart(section), strips, nc.scalar.copy)

        def window(section, row, j):
            lanes = SECTIONS[section][3] * PACK
            rows = part_rows(section)
            start = ((row % rows) * WIDTH + j) * lanes
            return spread[section, row // rows][:, start:start + OUT_WIDTH * lanes]

        grouped = keep.tile([P, TAPS, OUT_CH, PACK], BF16, name="grouped", align_bytes=64)
        weight_codes = keep.tile([P, TAPS * OUT_CH], U32, name="weight_codes", align_bytes=64)
        weight_scales = keep.tile([P, TAPS * OUT_CH], U8, name="weight_scales", align_bytes=64)
        by_tap = weight_rows[:].rearrange("o (p t k) -> o t k p", t=PACK, k=TAPS)
        banks = []

        def transpose_weights(bank):
            tap0 = TAPS_PER_BANK * bank
            turned = psum.tile([P, TAPS_PER_BANK * PACK, OUT_CH], BF16, name="bank")
            banks.append(turned)
            for k in range(min(TAPS_PER_BANK, TAPS - tap0)):
                for t in range(PACK):
                    nc.tensor.transpose(turned[:, k * PACK + t, :], by_tap[:, t, tap0 + k, :], identity[:])

        def group_weights(bank):
            tap0 = TAPS_PER_BANK * bank
            taps = min(TAPS_PER_BANK, TAPS - tap0)
            nc.scalar.copy(
                out=grouped[:, tap0:tap0 + taps, :, :],
                in_=banks[bank][:, 0:taps * PACK, :].rearrange("p (k t) o -> p k o t", t=PACK),
            )

        def quantise_weights(tap0, taps):
            nc.vector.quantize_mx(
                out=weight_codes[:, tap0 * OUT_CH:(tap0 + taps) * OUT_CH].bitcast(FP8X4),
                scales=weight_scales[:, tap0 * OUT_CH:(tap0 + taps) * OUT_CH],
                in_=grouped[:, tap0:tap0 + taps, :, :].rearrange("p k o t -> p (k o t)"),
            )

        load(0)
        load(1)
        load(2)
        nc.sync.dma_start(out=weight_rows[:], in_=weight)
        nc.sync.dma_start(out=bias_col[:], in_=bias)
        for section in range(3, len(SECTIONS)):
            load(section)

        regroup(0, 0, 0, 64, 0, 4, nc.vector.tensor_copy)
        regroup(0, 0, 64, 68, 0, 4, nc.vector.tensor_copy)
        regroup(0, 0, 0, 32, 4, 8, nc.vector.tensor_copy)
        regroup(0, 0, 32, 36, 4, 8, nc.vector.tensor_copy)
        regroup(0, 0, 36, 68, 4, 8, nc.scalar.copy)
        make_part(0, 1)

        for bank in range(WEIGHT_BANKS):
            transpose_weights(bank)

        make_part(1, 0)
        make_part(1, 1)
        make_part(2, 0)
        make_part(2, 1)
        make_part(2, 2)
        for bank in range(WEIGHT_BANKS):
            group_weights(bank)

        sums = {}
        results = {}

        def pass_columns(index):
            section, rows = SETS[index]
            columns = len(rows) * OUT_WIDTH * SECTIONS[section][3]
            return columns // 2 if index == len(SETS) - 1 else min(columns, BANK)

        def multiply(index, i, operands):
            section, rows = SETS[index]
            width = len(rows) * OUT_WIDTH * SECTIONS[section][3]
            step = pass_columns(index)
            if i == 0:
                sums[index] = []
                for start in range(0, width, step):
                    acc = psum.tile([P, BANK], F32, name="bank")
                    sums[index].append(acc)
            for j in range(3):
                tap = 3 * i + j
                codes, scales = operands[j]
                for part, acc in enumerate(sums[index]):
                    nc.tensor.matmul_mx(
                        out=acc[:, 0:step],
                        lhsT=weight_codes[:, tap * OUT_CH:(tap + 1) * OUT_CH].bitcast(FP8X4),
                        lhsT_scale=weight_scales[:, tap * OUT_CH:(tap + 1) * OUT_CH],
                        rhs=codes[:, part * step:(part + 1) * step].bitcast(FP8X4),
                        rhs_scale=scales[:, part * step:(part + 1) * step],
                        start=(tap == 0),
                        stop=(tap == TAPS - 1),
                    )
            if i == 2:
                finish(index)

        def finish(index):
            section, rows = SETS[index]
            n, row0, strip_rows, strips = SECTIONS[section]
            width = len(rows) * OUT_WIDTH * strips
            step = pass_columns(index)
            result = result_pool.tile([P, BANK], F32, name="result")
            by_strip = result[:, 0:width].rearrange("o (s q) -> o s q", s=strips)
            share = step // strips
            for part, acc in enumerate(sums[index]):
                nc.scalar.activation(
                    out=by_strip[:, :, part * share:(part + 1) * share],
                    in_=acc[:, 0:step].rearrange("o (q s) -> o s q", s=strips),
                    func=IDENTITY,
                    bias=bias_col[:, 0:1],
                )
            rows_out = out[n, :, row0:row0 + strips * strip_rows, :].rearrange("o (s r) u -> o s r u", r=strip_rows)
            nc.sync.dma_start(
                out=rows_out[:, :, rows[0]:rows[0] + len(rows), :].rearrange("o s r u -> o s (r u)"),
                in_=by_strip,
            )

        calls = [(index, i, k, j) for index in range(len(SETS)) for i in range(3)
                 for k in range(len(SETS[index][1])) for j in range(3)]
        first_use = {}
        clock = 0
        starts = []
        for index, i, k, j in calls:
            section, rows = SETS[index]
            first_use.setdefault((section, (rows[k] + i) // part_rows(section)), clock)
            starts.append(clock)
            clock += SECTIONS[section][3] // 8

        waiting = []
        weights_ready = False
        operands = []
        for call, now in zip(calls, starts):
            for key, use in first_use.items():
                if use <= now + LEAD and key not in spread:
                    make_part(*key)
            index, i, k, j = call
            section, rows = SETS[index]
            cols = OUT_WIDTH * SECTIONS[section][3]
            if k == 0:
                codes = slots_pool.tile([P, BANK], U32, name="codes", align_bytes=64)
                scales = slots_pool.tile([P, BANK], U8, name="scales", align_bytes=64)
                operands.append((codes, scales))
            share = cols // 2 if call == calls[-1] else cols
            for start in range(0, cols, share):
                nc.vector.quantize_mx(
                    out=operands[j][0][:, k * cols + start:k * cols + start + share].bitcast(FP8X4),
                    scales=operands[j][1][:, k * cols + start:k * cols + start + share],
                    in_=window(section, rows[k] + i, j)[:, start * PACK:(start + share) * PACK],
                )
            if j == 2 and k == len(rows) - 1:
                waiting.append((index, i, operands))
                operands = []
                if (index, i) == WEIGHTS_AFTER:
                    quantise_weights(0, 8)
                    quantise_weights(8, 1)
                    weights_ready = True
                for item in range(2 if weights_ready else 0):
                    if waiting:
                        multiply(*waiting.pop(0))
        for item in waiting:
            multiply(*item)
